import numpy as np
import ml_dtypes


def mxq(x, axis, fmt="e4m3"):
    dtype, down = {"e4m3": (ml_dtypes.float8_e4m3fn, 7), "e5m2": (ml_dtypes.float8_e5m2, 14)}[fmt]
    v = np.moveaxis(np.asarray(x, np.float32).astype(ml_dtypes.bfloat16).astype(np.float64), axis, -1)
    blocks = v.reshape(v.shape[:-1] + (-1, 32))
    amax = np.abs(blocks).max(-1, keepdims=True)
    byte = np.maximum(np.where(amax > 0, np.frexp(amax)[1] - 1 + 127, 0) - down, 1)
    scale = np.exp2(byte - 127.0)
    codes = (blocks / scale).astype(np.float32).astype(dtype).astype(np.float64)
    return np.moveaxis((codes * scale).reshape(v.shape), -1, axis)


WIDE = False


def mx_kscale(k):
    if not WIDE:
        return np.ones(k)
    levels = np.array([10, -10, 5, -5, 0])
    a = np.random.permutation(np.resize(levels, k // 512 * 4)).reshape(k // 512, 4)
    idx = np.arange(k)
    return np.exp2(a[idx // 512, idx % 128 // 32])


BF16 = ml_dtypes.bfloat16


def bf(x):
    return np.asarray(x, np.float32).astype(BF16)


def f64(x):
    return np.asarray(x).astype(np.float64)


E2M1 = np.array([0.0, 0.5, 1.0, 1.5, 2.0, 3.0, 4.0, 6.0, -0.0, -0.5, -1.0, -1.5, -2.0, -3.0, -4.0, -6.0])


def pack_weight(w, fmt):
    k, n = w.shape
    w = f64(bf(w)).reshape(k // 32, 32, n)
    amax = np.abs(w).max(1)
    if fmt == "e4m3":
        byte = np.frexp(amax)[1] - 1 + 127 - 7
    else:
        mant, ex = np.frexp(amax / 6.0)
        byte = np.where(mant > 0.5, ex, ex - 1) + 127
    byte = np.clip(np.where(amax > 0, byte, 1), 1, 254)
    scaled = (w * np.exp2(127.0 - byte)[:, None, :]).reshape(k, n).astype(np.float32)
    by_word = np.ascontiguousarray(scaled.reshape(k // 512, 128, 4, n).transpose(0, 1, 3, 2))
    if fmt == "e4m3":
        words = by_word.astype(ml_dtypes.float8_e4m3fn).view(np.uint8)
    else:
        c = by_word.astype(ml_dtypes.float4_e2m1fn).view(np.uint8) & 0xF
        words = c[..., 0::2] | (c[..., 1::2] << 4)
    return np.ascontiguousarray(words), np.ascontiguousarray(byte.astype(np.uint8).reshape(k // 512, 16, n))


def unpack_weight(words, scales, fmt):
    g, p, n, _ = words.shape
    if fmt == "e4m3":
        vals = np.ascontiguousarray(words).view(ml_dtypes.float8_e4m3fn).astype(np.float64)
    else:
        nib = np.empty((g, p, n, 4), np.uint8)
        nib[..., 0::2] = words & 0xF
        nib[..., 1::2] = words >> 4
        vals = E2M1[nib]
    vals = vals * np.repeat(np.exp2(scales.astype(np.float64) - 127.0), 8, axis=1)[..., None]
    return vals.transpose(0, 1, 3, 2).reshape(g * 512, n)


B, C, H, W, RQ, RV = 1, 512, 64, 64, 4, 1
DQ, DV = C // RQ, C // RV
N = H * W
M = (H // 2) * (W // 2)
FMT = "e4m3"


def setup_inputs():
    t = mx_kscale(DV)
    q = bf(np.random.standard_normal((B, DQ, N)) * 8.0 / np.sqrt(DQ))
    k_pool = bf(0.5 + 0.35 * np.random.standard_normal((B, DQ, M)))
    v_pool = bf((0.5 + 0.35 * np.random.standard_normal((B, DV, M))) * t[None, :, None])
    imgs = bf(np.random.standard_normal((B, C, H, W)))
    w_out = np.random.standard_normal((C, DV)) * 1.5 / np.sqrt(DV) / t[None, :]
    words, scales = pack_weight(np.ascontiguousarray(w_out.T), FMT)
    gain = bf(1.0 + 0.1 * np.random.standard_normal(1))
    return {"q": q,
            "k_pool": k_pool,
            "v_pool": v_pool,
            "imgs": imgs,
            "w_out_words": words,
            "w_out_scales": scales,
            "gain": gain}


def reference(q, k_pool, v_pool, imgs, w_out_words, w_out_scales, gain):
    s = f64(q).transpose(0, 2, 1) @ f64(k_pool)
    e = np.exp(s - s.max(-1, keepdims=True))
    att = (mxq(e, 2, "e4m3") @ mxq(f64(v_pool), 2, "e4m3").transpose(0, 2, 1)) / e.sum(-1, keepdims=True)
    y = mxq(att, 2, "e4m3") @ unpack_weight(w_out_words, w_out_scales, FMT)
    return f64(imgs) + y.transpose(0, 2, 1).reshape(B, C, H, W) * f64(gain)

@@ -1,0 +1,309 @@
+from contextlib import ExitStack
+
+import concourse.mybir as mybir
+from concourse.masks import make_identity
+
+F32 = mybir.dt.float32
+BF16 = mybir.dt.bfloat16
+I32 = mybir.dt.int32
+U32 = mybir.dt.uint32
+U8 = mybir.dt.uint8
+FP8X4 = mybir.dt.float8_e4m3fn_x4
+ALU = mybir.AluOpType
+ACT = mybir.ActivationFunctionType
+AXIS_X = mybir.AxisListType.X
+
+P = 128
+PACK = 4
+K_PASS = P * PACK
+BANK = 512
+
+N_PIX = 4096
+N_POS = 1024
+D_QK = 128
+D_V = 512
+C_OUT = 512
+
+N_TILES = N_PIX // P
+GROUP = 4
+N_GROUPS = N_TILES // GROUP
+POS_PASSES = N_POS // K_PASS
+POS_HALVES = N_POS // BANK
+V_BLOCKS = D_V // P
+C_BLOCKS = C_OUT // P
+
+ATTEND_LAG = 5
+
+FLOPS = 2 * N_PIX * N_POS * D_QK + 2 * N_PIX * N_POS * D_V + 2 * N_PIX * D_V * C_OUT
+
+
+def tile_selfattentionconv2d_pb_t_kernel(
+    tc, q, k_pool, v_pool, imgs, w_out_words, w_out_scales, gain, out
+):
+    nc = tc.nc
+    with ExitStack() as stack:
+        keep = stack.enter_context(tc.tile_pool(name="keep", bufs=1))
+        small = stack.enter_context(tc.tile_pool(name="small", bufs=4))
+        stream = stack.enter_context(tc.tile_pool(name="stream", bufs=3))
+        packed = stack.enter_context(tc.tile_pool(name="packed", bufs=ATTEND_LAG + 2))
+        results = stack.enter_context(tc.tile_pool(name="results", bufs=4))
+        psum_scores = stack.enter_context(tc.psum_pool(name="psum_scores", bufs=2))
+        psum_one = stack.enter_context(tc.psum_pool(name="psum_one", bufs=1))
+        psum_two = stack.enter_context(tc.psum_pool(name="psum_two", bufs=2))
+
+        k_sb = keep.tile([P, N_POS], BF16)
+        nc.sync.dma_start(out=k_sb[:], in_=k_pool.rearrange("b d m -> (b d) m"))
+        q_sb = keep.tile([P, N_PIX], BF16)
+        q_rows = q.rearrange("b d n -> (b d) n")
+        first = GROUP * P
+        nc.sync.dma_start(out=q_sb[:, :first], in_=q_rows[:, :first])
+        v_sb = keep.tile([P, PACK, N_POS], BF16)
+        nc.sync.dma_start(out=v_sb[:], in_=v_pool.rearrange("b (j t) m -> (b j) t m", t=PACK))
+        nc.sync.dma_start(out=q_sb[:, first:], in_=q_rows[:, first:])
+        gain_bf = keep.tile([P, 1], BF16)
+        nc.sync.dma_start(out=gain_bf[:], in_=gain.partition_broadcast(P))
+        w_words = keep.tile([P, C_OUT * PACK], U8, align_bytes=64)
+        nc.sync.dma_start(
+            out=w_words[:].bitcast(I32),
+            in_=w_out_words.rearrange("g p c t -> (g p) (c t)").bitcast(I32),
+        )
+        w_scales = keep.tile([P, C_OUT], U8, align_bytes=64)
+        nc.vector.memset(w_scales[:].bitcast(I32), 0)
+        scale_rows = w_out_scales.rearrange("g r c -> (g r) c")
+        for quadrant in range(4):
+            nc.sync.dma_start(
+                out=w_scales[32 * quadrant : 32 * quadrant + 4, :].bitcast(I32),
+                in_=scale_rows[4 * quadrant : 4 * quadrant + 4, :].bitcast(I32),
+            )
+        imgs_sb = keep.tile([P, C_BLOCKS, N_PIX], BF16)
+        imgs_rows = imgs.rearrange("b (cb c) h w -> c (b cb) (h w)", c=P)
+        for cb in range(C_BLOCKS):
+            nc.sync.dma_start(out=imgs_sb[:, cb, :], in_=imgs_rows[:, cb, :])
+        out_rows = out.rearrange("b (cb c) h w -> c (b cb) (h w)", c=P)
+
+        ident = keep.tile([P, P], F32)
+        make_identity(nc, ident[:])
+        gain_f32 = keep.tile([P, 1], F32)
+        nc.vector.tensor_copy(out=gain_f32[:], in_=gain_bf[:])
+
+        k_sorted = keep.tile([P, N_POS], BF16)
+        nc.vector.tensor_copy(
+            out=k_sorted[:].bitcast(F32).rearrange("d (g u p) -> d g u p", g=POS_PASSES, u=2),
+            in_=k_sb[:].bitcast(F32).rearrange("d (g p u) -> d g u p", g=POS_PASSES, u=2),
+        )
+
+        v_grouped = keep.tile([P, POS_PASSES, V_BLOCKS, P, PACK], BF16, align_bytes=64)
+        v_grouped_words = v_grouped[:].rearrange("p g t j k -> p (g t j k)").bitcast(F32)
+        v_grouped_words = v_grouped_words.rearrange(
+            "p (g t j u) -> p g t j u", g=POS_PASSES, t=V_BLOCKS, u=2
+        )
+        for t in range(V_BLOCKS):
+            v_words_in = v_sb[:, t, :].bitcast(F32)
+            vT_ps = psum_two.tile([P, POS_PASSES * 2, P], F32, tag="bank")
+            for g in range(POS_PASSES):
+                for u in range(2):
+                    nc.tensor.transpose(
+                        vT_ps[:, 2 * g + u, :],
+                        v_words_in[:, 256 * g + u : 256 * (g + 1) : 2],
+                        ident[:],
+                    )
+            nc.vector.tensor_copy(
+                out=v_grouped_words[:, :, t, :, :],
+                in_=vT_ps[:].rearrange("p (g u) j -> p g j u", u=2),
+            )
+        v_codes = keep.tile([P, POS_PASSES, V_BLOCKS, P], U32, align_bytes=64)
+        v_scales = keep.tile([P, POS_PASSES, V_BLOCKS, P], U8, align_bytes=64)
+        nc.vector.quantize_mx(
+            out=v_codes[:].rearrange("p g t j -> p (g t j)").bitcast(FP8X4),
+            scales=v_scales[:].rearrange("p g t j -> p (g t j)"),
+            in_=v_grouped[:].rearrange("p g t j k -> p (g t j k)"),
+        )
+
+        score_banks = {}
+        neg_max = {}
+        e_rows = {}
+        e_sums = {}
+        e_banks = {}
+        e_grouped = {}
+        e_packed = {}
+        inv_sum = {}
+        att_banks = {}
+        att_grouped = {}
+        att_packed = {}
+        y_banks = {}
+
+        def scores(i):
+            halves = []
+            for h in range(POS_HALVES):
+                s_ps = psum_scores.tile([P, BANK], F32, name="s_ps%d" % h)
+                nc.tensor.matmul(
+                    out=s_ps[:],
+                    lhsT=q_sb[:, P * i : P * (i + 1)],
+                    rhs=k_sorted[:, BANK * h : BANK * (h + 1)],
+                    start=True,
+                    stop=True,
+                )
+                halves.append(s_ps)
+            score_banks[i] = halves
+
+        def row_max(i):
+            half_max = small.tile([P, POS_HALVES], F32)
+            for h in range(POS_HALVES):
+                nc.vector.reduce_max(out=half_max[:, h : h + 1], in_=score_banks[i][h][:], axis=AXIS_X)
+            minus_max = small.tile([P, 1], F32)
+            nc.vector.tensor_scalar(
+                out=minus_max[:],
+                in0=half_max[:, 0:1],
+                scalar1=half_max[:, 1:2],
+                scalar2=-1.0,
+                op0=ALU.max,
+                op1=ALU.mult,
+            )
+            neg_max[i] = minus_max
+
+        def exponentials(i):
+            group, member = divmod(i, GROUP)
+            if member == 0:
+                e_sums[group] = small.tile([P, GROUP, POS_HALVES], F32, name="sums")
+            e_bf = stream.tile([P, N_POS], BF16)
+            for h in range(POS_HALVES):
+                nc.scalar.activation(
+                    out=e_bf[:, BANK * h : BANK * (h + 1)],
+                    in_=score_banks[i][h][:],
+                    func=ACT.Exp,
+                    bias=neg_max[i][:, 0:1],
+                    scale=1.0,
+                    accum_out=e_sums[group][:, member, h : h + 1],
+                )
+            e_rows[i] = e_bf
+
+        def transpose_e(i):
+            eT_ps = psum_one.tile([P, POS_PASSES * 2, P], F32)
+            words = e_rows[i][:].bitcast(F32)
+            for b in range(POS_PASSES * 2):
+                nc.tensor.transpose(eT_ps[:, b, :], words[:, P * b : P * (b + 1)], ident[:])
+            e_banks[i] = eT_ps
+
+        def regroup_e(i):
+            e_grp = stream.tile([P, POS_PASSES * P * PACK], BF16, align_bytes=64)
+            nc.scalar.copy(
+                out=e_grp[:].bitcast(F32).rearrange("p (g n u) -> p g n u", g=POS_PASSES, u=2),
+                in_=e_banks[i][:].rearrange("p (g u) n -> p g n u", u=2),
+            )
+            e_grouped[i] = e_grp
+
+        def quantise_e(i):
+            e_codes = packed.tile([P, POS_PASSES, P], U32, align_bytes=64)
+            e_scales = packed.tile([P, POS_PASSES, P], U8, align_bytes=64)
+            nc.vector.quantize_mx(
+                out=e_codes[:].rearrange("p g n -> p (g n)").bitcast(FP8X4),
+                scales=e_scales[:].rearrange("p g n -> p (g n)"),
+                in_=e_grouped[i][:],
+            )
+            e_packed[i] = (e_codes, e_scales)
+
+        def spread_row_sums(group):
+            row_sum = small.tile([P, GROUP], F32)
+            nc.vector.reduce_sum(out=row_sum[:], in_=e_sums[group][:], axis=AXIS_X)
+            inverse = small.tile([P, GROUP], F32)
+            nc.vector.reciprocal(out=inverse[:], in_=row_sum[:])
+            inv_ps = psum_two.tile([P, GROUP, P], F32, tag="bank")
+            for member in range(GROUP):
+                nc.tensor.transpose(
+                    inv_ps[:, member, :], inverse[:, member : member + 1].to_broadcast([P, P]), ident[:]
+                )
+            inv_sb = stream.tile([P, GROUP, P], F32)
+            nc.scalar.copy(out=inv_sb[:], in_=inv_ps[:])
+            inv_sum[group] = inv_sb
+
+        def attend(i):
+            e_codes, e_scales = e_packed[i]
+            att_ps = psum_one.tile([P, V_BLOCKS, P], F32)
+            for t in range(V_BLOCKS):
+                for g in range(POS_PASSES):
+                    nc.tensor.matmul_mx(
+                        out=att_ps[:, t, :],
+                        lhsT=v_codes[:, g, t, :].bitcast(FP8X4),
+                        lhsT_scale=v_scales[:, g, t, :],
+                        rhs=e_codes[:, g, :].bitcast(FP8X4),
+                        rhs_scale=e_scales[:, g, :],
+                        start=(g == 0),
+                        stop=(g == POS_PASSES - 1),
+                    )
+            att_banks[i] = att_ps
+
+        def normalise(i):
+            group, member = divmod(i, GROUP)
+            if member == 0:
+                att_grouped[group] = stream.tile([P, GROUP, P, PACK], BF16, name="att_grp", align_bytes=64)
+            nc.vector.tensor_tensor(
+                out=att_grouped[group][:, member, :, :],
+                in0=att_banks[i][:].rearrange("p t n -> p n t"),
+                in1=inv_sum[group][:, member, :].unsqueeze(2).to_broadcast([P, P, PACK]),
+                op=ALU.mult,
+            )
+
+        def quantise_att(group):
+            att_codes = stream.tile([P, GROUP * P], U32, align_bytes=64)
+            att_scales = stream.tile([P, GROUP * P], U8, align_bytes=64)
+            nc.vector.quantize_mx(
+                out=att_codes[:].bitcast(FP8X4),
+                scales=att_scales[:],
+                in_=att_grouped[group][:].rearrange("p m n t -> p (m n t)"),
+            )
+            att_packed[group] = (att_codes, att_scales)
+
+        def project(group, cb):
+            att_codes, att_scales = att_packed[group]
+            y_ps = psum_two.tile([P, GROUP * P], F32, tag="bank")
+            nc.tensor.matmul_mx(
+                out=y_ps[:],
+                lhsT=w_words[:, P * PACK * cb : P * PACK * (cb + 1)].bitcast(FP8X4),
+                lhsT_scale=w_scales[:, P * cb : P * (cb + 1)],
+                rhs=att_codes[:].bitcast(FP8X4),
+                rhs_scale=att_scales[:],
+                start=True,
+                stop=True,
+            )
+            y_banks[(group, cb)] = y_ps
+
+        def residual(group, cb):
+            pixels = slice(GROUP * P * group, GROUP * P * (group + 1))
+            o_sb = results.tile([P, GROUP * P], F32)
+            nc.vector.scalar_tensor_tensor(
+                out=o_sb[:],
+                in0=y_banks[(group, cb)][:],
+                scalar=gain_f32[:, 0:1],
+                in1=imgs_sb[:, cb, pixels],
+                op0=ALU.mult,
+                op1=ALU.add,
+            )
+            nc.sync.dma_start(out=out_rows[:, cb, pixels], in_=o_sb[:])
+
+        def is_tile(i):
+            return 0 <= i < N_TILES
+
+        for step in range(-1, N_TILES + ATTEND_LAG + GROUP):
+            if is_tile(step - ATTEND_LAG):
+                attend(step - ATTEND_LAG)
+            group, cb = divmod(step - ATTEND_LAG - GROUP, GROUP)
+            if 0 <= group < N_GROUPS:
+                project(group, cb)
+            if is_tile(step + 1):
+                scores(step + 1)
+            if is_tile(step):
+                row_max(step)
+            if is_tile(step - 1):
+                exponentials(step - 1)
+                transpose_e(step - 1)
+                regroup_e(step - 1)
+            if is_tile(step - ATTEND_LAG):
+                normalise(step - ATTEND_LAG)
+            if is_tile(step - 2):
+                quantise_e(step - 2)
+            if is_tile(step - 1) and (step - 1) % GROUP == GROUP - 1:
+                spread_row_sums((step - 1) // GROUP)
+            if is_tile(step - ATTEND_LAG) and (step - ATTEND_LAG) % GROUP == GROUP - 1:
+                quantise_att((step - ATTEND_LAG) // GROUP)
+            if 0 <= group < N_GROUPS:
+                residual(group, cb)

@@ -25,14 +25,14 @@ D_V = 512
 C_OUT = 512
 
 N_TILES = N_PIX // P
-GROUP = 4
-N_GROUPS = N_TILES // GROUP
+GROUP = 2
+GROUP_PIX = GROUP * P
 POS_PASSES = N_POS // K_PASS
 POS_HALVES = N_POS // BANK
 V_BLOCKS = D_V // P
 C_BLOCKS = C_OUT // P
-
-ATTEND_LAG = 5
+UNIT_BLOCKS = BANK // GROUP_PIX
+V_ROUNDS_A_STEP = 2
 
 FLOPS = 2 * N_PIX * N_POS * D_QK + 2 * N_PIX * N_POS * D_V + 2 * N_PIX * D_V * C_OUT
 
@@ -42,10 +42,11 @@ def tile_selfattentionconv2d_pb_t_kernel(
 ):
     nc = tc.nc
     with ExitStack() as stack:
+        stack.enter_context(tc.manual_schedule())
         keep = stack.enter_context(tc.tile_pool(name="keep", bufs=1))
         small = stack.enter_context(tc.tile_pool(name="small", bufs=4))
         stream = stack.enter_context(tc.tile_pool(name="stream", bufs=3))
-        packed = stack.enter_context(tc.tile_pool(name="packed", bufs=ATTEND_LAG + 2))
+        packed = stack.enter_context(tc.tile_pool(name="packed", bufs=4))
         results = stack.enter_context(tc.tile_pool(name="results", bufs=4))
         psum_scores = stack.enter_context(tc.psum_pool(name="psum_scores", bufs=2))
         psum_one = stack.enter_context(tc.psum_pool(name="psum_one", bufs=1))
@@ -55,7 +56,7 @@ def tile_selfattentionconv2d_pb_t_kernel(
         nc.sync.dma_start(out=k_sb[:], in_=k_pool.rearrange("b d m -> (b d) m"))
         q_sb = keep.tile([P, N_PIX], BF16)
         q_rows = q.rearrange("b d n -> (b d) n")
-        first = GROUP * P
+        first = N_PIX // 4
         nc.sync.dma_start(out=q_sb[:, :first], in_=q_rows[:, :first])
         v_sb = keep.tile([P, PACK, N_POS], BF16)
         nc.sync.dma_start(out=v_sb[:], in_=v_pool.rearrange("b (j t) m -> (b j) t m", t=PACK))
@@ -84,7 +85,7 @@ def tile_selfattentionconv2d_pb_t_kernel(
         ident = keep.tile([P, P], F32)
         make_identity(nc, ident[:])
         gain_f32 = keep.tile([P, 1], F32)
-        nc.vector.tensor_copy(out=gain_f32[:], in_=gain_bf[:])
+        nc.gpsimd.tensor_copy(out=gain_f32[:], in_=gain_bf[:])
 
         k_sorted = keep.tile([P, N_POS], BF16)
         nc.vector.tensor_copy(
@@ -97,7 +98,10 @@ def tile_selfattentionconv2d_pb_t_kernel(
         v_grouped_words = v_grouped_words.rearrange(
             "p (g t j u) -> p g t j u", g=POS_PASSES, t=V_BLOCKS, u=2
         )
-        for t in range(V_BLOCKS):
+        v_codes = keep.tile([P, POS_PASSES, V_BLOCKS, P], U32, align_bytes=64)
+        v_scales = keep.tile([P, POS_PASSES, V_BLOCKS, P], U8, align_bytes=64)
+
+        def transpose_v(t):
             v_words_in = v_sb[:, t, :].bitcast(F32)
             vT_ps = psum_two.tile([P, POS_PASSES * 2, P], F32, tag="bank")
             for g in range(POS_PASSES):
@@ -111,55 +115,58 @@ def tile_selfattentionconv2d_pb_t_kernel(
                 out=v_grouped_words[:, :, t, :, :],
                 in_=vT_ps[:].rearrange("p (g u) j -> p g j u", u=2),
             )
-        v_codes = keep.tile([P, POS_PASSES, V_BLOCKS, P], U32, align_bytes=64)
-        v_scales = keep.tile([P, POS_PASSES, V_BLOCKS, P], U8, align_bytes=64)
-        nc.vector.quantize_mx(
-            out=v_codes[:].rearrange("p g t j -> p (g t j)").bitcast(FP8X4),
-            scales=v_scales[:].rearrange("p g t j -> p (g t j)"),
-            in_=v_grouped[:].rearrange("p g t j k -> p (g t j k)"),
-        )
+
+        def quantise_v():
+            nc.vector.quantize_mx(
+                out=v_codes[:].rearrange("p g t j -> p (g t j)").bitcast(FP8X4),
+                scales=v_scales[:].rearrange("p g t j -> p (g t j)"),
+                in_=v_grouped[:].rearrange("p g t j k -> p (g t j k)"),
+            )
 
         score_banks = {}
+        half_maxima = {}
         neg_max = {}
         e_rows = {}
         e_sums = {}
         e_banks = {}
         e_grouped = {}
         e_packed = {}
-        inv_sum = {}
+        inverses = {}
+        inv_banks = {}
+        inv_spread = {}
         att_banks = {}
         att_grouped = {}
         att_packed = {}
         y_banks = {}
 
-        def scores(i):
-            halves = []
-            for h in range(POS_HALVES):
-                s_ps = psum_scores.tile([P, BANK], F32, name="s_ps%d" % h)
-                nc.tensor.matmul(
-                    out=s_ps[:],
-                    lhsT=q_sb[:, P * i : P * (i + 1)],
-                    rhs=k_sorted[:, BANK * h : BANK * (h + 1)],
-                    start=True,
-                    stop=True,
-                )
-                halves.append(s_ps)
-            score_banks[i] = halves
+        def scores(i, h):
+            s_ps = psum_scores.tile([P, BANK], F32, name="s_ps%d" % h)
+            nc.tensor.matmul(
+                out=s_ps[:],
+                lhsT=q_sb[:, P * i : P * (i + 1)],
+                rhs=k_sorted[:, BANK * h : BANK * (h + 1)],
+                start=True,
+                stop=True,
+            )
+            score_banks[(i, h)] = s_ps
 
-        def row_max(i):
-            half_max = small.tile([P, POS_HALVES], F32)
+        def half_max(i):
+            maxima = small.tile([P, POS_HALVES], F32)
             for h in range(POS_HALVES):
-                nc.vector.reduce_max(out=half_max[:, h : h + 1], in_=score_banks[i][h][:], axis=AXIS_X)
-            minus_max = small.tile([P, 1], F32)
+                nc.vector.reduce_max(out=maxima[:, h : h + 1], in_=score_banks[(i, h)][:], axis=AXIS_X)
+            half_maxima[i] = maxima
+
+        def minus_max(i):
+            negated = small.tile([P, 1], F32)
             nc.vector.tensor_scalar(
-                out=minus_max[:],
-                in0=half_max[:, 0:1],
-                scalar1=half_max[:, 1:2],
+                out=negated[:],
+                in0=half_maxima[i][:, 0:1],
+                scalar1=half_maxima[i][:, 1:2],
                 scalar2=-1.0,
                 op0=ALU.max,
                 op1=ALU.mult,
             )
-            neg_max[i] = minus_max
+            neg_max[i] = negated
 
         def exponentials(i):
             group, member = divmod(i, GROUP)
@@ -169,7 +176,7 @@ def tile_selfattentionconv2d_pb_t_kernel(
             for h in range(POS_HALVES):
                 nc.scalar.activation(
                     out=e_bf[:, BANK * h : BANK * (h + 1)],
-                    in_=score_banks[i][h][:],
+                    in_=score_banks[(i, h)][:],
                     func=ACT.Exp,
                     bias=neg_max[i][:, 0:1],
                     scale=1.0,
@@ -202,19 +209,27 @@ def tile_selfattentionconv2d_pb_t_kernel(
             )
             e_packed[i] = (e_codes, e_scales)
 
-        def spread_row_sums(group):
+        def invert_row_sums(group):
             row_sum = small.tile([P, GROUP], F32)
             nc.vector.reduce_sum(out=row_sum[:], in_=e_sums[group][:], axis=AXIS_X)
             inverse = small.tile([P, GROUP], F32)
             nc.vector.reciprocal(out=inverse[:], in_=row_sum[:])
+            inverses[group] = inverse
+
+        def transpose_inverses(group):
             inv_ps = psum_two.tile([P, GROUP, P], F32, tag="bank")
             for member in range(GROUP):
                 nc.tensor.transpose(
-                    inv_ps[:, member, :], inverse[:, member : member + 1].to_broadcast([P, P]), ident[:]
+                    inv_ps[:, member, :],
+                    inverses[group][:, member : member + 1].to_broadcast([P, P]),
+                    ident[:],
                 )
+            inv_banks[group] = inv_ps
+
+        def copy_inverses(group):
             inv_sb = stream.tile([P, GROUP, P], F32)
-            nc.scalar.copy(out=inv_sb[:], in_=inv_ps[:])
-            inv_sum[group] = inv_sb
+            nc.scalar.copy(out=inv_sb[:], in_=inv_banks[group][:])
+            inv_spread[group] = inv_sb
 
         def attend(i):
             e_codes, e_scales = e_packed[i]
@@ -239,13 +254,13 @@ def tile_selfattentionconv2d_pb_t_kernel(
             nc.vector.tensor_tensor(
                 out=att_grouped[group][:, member, :, :],
                 in0=att_banks[i][:].rearrange("p t n -> p n t"),
-                in1=inv_sum[group][:, member, :].unsqueeze(2).to_broadcast([P, P, PACK]),
+                in1=inv_spread[group][:, member, :].unsqueeze(2).to_broadcast([P, P, PACK]),
                 op=ALU.mult,
             )
 
         def quantise_att(group):
-            att_codes = stream.tile([P, GROUP * P], U32, align_bytes=64)
-            att_scales = stream.tile([P, GROUP * P], U8, align_bytes=64)
+            att_codes = stream.tile([P, GROUP_PIX], U32, align_bytes=64)
+            att_scales = stream.tile([P, GROUP_PIX], U8, align_bytes=64)
             nc.vector.quantize_mx(
                 out=att_codes[:].bitcast(FP8X4),
                 scales=att_scales[:],
@@ -253,57 +268,79 @@ def tile_selfattentionconv2d_pb_t_kernel(
             )
             att_packed[group] = (att_codes, att_scales)
 
-        def project(group, cb):
+        def project(group, unit):
             att_codes, att_scales = att_packed[group]
-            y_ps = psum_two.tile([P, GROUP * P], F32, tag="bank")
-            nc.tensor.matmul_mx(
-                out=y_ps[:],
-                lhsT=w_words[:, P * PACK * cb : P * PACK * (cb + 1)].bitcast(FP8X4),
-                lhsT_scale=w_scales[:, P * cb : P * (cb + 1)],
-                rhs=att_codes[:].bitcast(FP8X4),
-                rhs_scale=att_scales[:],
-                start=True,
-                stop=True,
-            )
-            y_banks[(group, cb)] = y_ps
+            y_ps = psum_two.tile([P, UNIT_BLOCKS, GROUP_PIX], F32, tag="bank")
+            for b in range(UNIT_BLOCKS):
+                cb = UNIT_BLOCKS * unit + b
+                nc.tensor.matmul_mx(
+                    out=y_ps[:, b, :],
+                    lhsT=w_words[:, P * PACK * cb : P * PACK * (cb + 1)].bitcast(FP8X4),
+                    lhsT_scale=w_scales[:, P * cb : P * (cb + 1)],
+                    rhs=att_codes[:].bitcast(FP8X4),
+                    rhs_scale=att_scales[:],
+                    start=True,
+                    stop=True,
+                )
+            y_banks[(group, unit)] = y_ps
 
-        def residual(group, cb):
-            pixels = slice(GROUP * P * group, GROUP * P * (group + 1))
-            o_sb = results.tile([P, GROUP * P], F32)
-            nc.vector.scalar_tensor_tensor(
-                out=o_sb[:],
-                in0=y_banks[(group, cb)][:],
-                scalar=gain_f32[:, 0:1],
-                in1=imgs_sb[:, cb, pixels],
-                op0=ALU.mult,
-                op1=ALU.add,
-            )
-            nc.sync.dma_start(out=out_rows[:, cb, pixels], in_=o_sb[:])
+        def residual(group, unit):
+            blocks = slice(UNIT_BLOCKS * unit, UNIT_BLOCKS * (unit + 1))
+            pixels = slice(GROUP_PIX * group, GROUP_PIX * (group + 1))
+            o_sb = results.tile([P, UNIT_BLOCKS, GROUP_PIX], F32)
+            if group == N_TILES // GROUP - 1:
+                nc.vector.scalar_tensor_tensor(
+                    out=o_sb[:],
+                    in0=y_banks[(group, unit)][:],
+                    scalar=gain_f32[:, 0:1],
+                    in1=imgs_sb[:, blocks, pixels],
+                    op0=ALU.mult,
+                    op1=ALU.add,
+                )
+            else:
+                nc.scalar.activation(
+                    out=o_sb[:], in_=y_banks[(group, unit)][:], func=ACT.Copy, scale=gain_f32[:, 0:1]
+                )
+                nc.gpsimd.tensor_tensor(out=o_sb[:], in0=o_sb[:], in1=imgs_sb[:, blocks, pixels], op=ALU.add)
+            nc.sync.dma_start(out=out_rows[:, blocks, pixels], in_=o_sb[:])
 
         def is_tile(i):
             return 0 <= i < N_TILES
 
-        for step in range(-1, N_TILES + ATTEND_LAG + GROUP):
-            if is_tile(step - ATTEND_LAG):
-                attend(step - ATTEND_LAG)
-            group, cb = divmod(step - ATTEND_LAG - GROUP, GROUP)
-            if 0 <= group < N_GROUPS:
-                project(group, cb)
+        def closes_group(i):
+            return is_tile(i) and i % GROUP == GROUP - 1
+
+        for step in range(-1, N_TILES + 5):
+            if closes_group(step - 2):
+                invert_row_sums((step - 2) // GROUP)
+                transpose_inverses((step - 2) // GROUP)
+            if is_tile(step - 5):
+                project((step - 5) // GROUP, (step - 5) % GROUP)
+            if is_tile(step - 3):
+                attend(step - 3)
             if is_tile(step + 1):
-                scores(step + 1)
-            if is_tile(step):
-                row_max(step)
+                scores(step + 1, 0)
+                scores(step + 1, 1)
             if is_tile(step - 1):
                 exponentials(step - 1)
                 transpose_e(step - 1)
-                regroup_e(step - 1)
-            if is_tile(step - ATTEND_LAG):
-                normalise(step - ATTEND_LAG)
+            if is_tile(step - 2):
+                regroup_e(step - 2)
+            if closes_group(step - 2):
+                copy_inverses((step - 2) // GROUP)
+            if is_tile(step):
+                half_max(step)
+                minus_max(step)
             if is_tile(step - 2):
                 quantise_e(step - 2)
-            if is_tile(step - 1) and (step - 1) % GROUP == GROUP - 1:
-                spread_row_sums((step - 1) // GROUP)
-            if is_tile(step - ATTEND_LAG) and (step - ATTEND_LAG) % GROUP == GROUP - 1:
-                quantise_att((step - ATTEND_LAG) // GROUP)
-            if 0 <= group < N_GROUPS:
-                residual(group, cb)
+            if is_tile(step - 5):
+                residual((step - 5) // GROUP, (step - 5) % GROUP)
+            if is_tile(step - 3):
+                normalise(step - 3)
+            if closes_group(step - 3):
+                quantise_att((step - 3) // GROUP)
+            if step in (1, 2):
+                for t in range(V_ROUNDS_A_STEP * (step - 1), V_ROUNDS_A_STEP * step):
+                    transpose_v(t)
+            if step == 2:
+                quantise_v()

@@ -25,14 +25,14 @@ D_V = 512
 C_OUT = 512
 
 N_TILES = N_PIX // P
-GROUP = 2
-GROUP_PIX = GROUP * P
+GROUP = 4
+N_GROUPS = N_TILES // GROUP
 POS_PASSES = N_POS // K_PASS
 POS_HALVES = N_POS // BANK
 V_BLOCKS = D_V // P
 C_BLOCKS = C_OUT // P
-UNIT_BLOCKS = BANK // GROUP_PIX
-V_ROUNDS_A_STEP = 2
+
+ATTEND_LAG = 5
 
 FLOPS = 2 * N_PIX * N_POS * D_QK + 2 * N_PIX * N_POS * D_V + 2 * N_PIX * D_V * C_OUT
 
@@ -42,21 +42,19 @@ def tile_selfattentionconv2d_pb_t_kernel(
 ):
     nc = tc.nc
     with ExitStack() as stack:
-        stack.enter_context(tc.manual_schedule())
         keep = stack.enter_context(tc.tile_pool(name="keep", bufs=1))
         small = stack.enter_context(tc.tile_pool(name="small", bufs=4))
         stream = stack.enter_context(tc.tile_pool(name="stream", bufs=3))
-        packed = stack.enter_context(tc.tile_pool(name="packed", bufs=4))
+        packed = stack.enter_context(tc.tile_pool(name="packed", bufs=ATTEND_LAG + 2))
         results = stack.enter_context(tc.tile_pool(name="results", bufs=4))
         psum_scores = stack.enter_context(tc.psum_pool(name="psum_scores", bufs=2))
-        psum_one = stack.enter_context(tc.psum_pool(name="psum_one", bufs=1))
-        psum_two = stack.enter_context(tc.psum_pool(name="psum_two", bufs=2))
+        psum_shared = stack.enter_context(tc.psum_pool(name="psum_shared", bufs=4))
 
         k_sb = keep.tile([P, N_POS], BF16)
         nc.sync.dma_start(out=k_sb[:], in_=k_pool.rearrange("b d m -> (b d) m"))
         q_sb = keep.tile([P, N_PIX], BF16)
         q_rows = q.rearrange("b d n -> (b d) n")
-        first = N_PIX // 4
+        first = GROUP * P
         nc.sync.dma_start(out=q_sb[:, :first], in_=q_rows[:, :first])
         v_sb = keep.tile([P, PACK, N_POS], BF16)
         nc.sync.dma_start(out=v_sb[:], in_=v_pool.rearrange("b (j t) m -> (b j) t m", t=PACK))
@@ -85,7 +83,7 @@ def tile_selfattentionconv2d_pb_t_kernel(
         ident = keep.tile([P, P], F32)
         make_identity(nc, ident[:])
         gain_f32 = keep.tile([P, 1], F32)
-        nc.gpsimd.tensor_copy(out=gain_f32[:], in_=gain_bf[:])
+        nc.vector.tensor_copy(out=gain_f32[:], in_=gain_bf[:])
 
         k_sorted = keep.tile([P, N_POS], BF16)
         nc.vector.tensor_copy(
@@ -98,12 +96,9 @@ def tile_selfattentionconv2d_pb_t_kernel(
         v_grouped_words = v_grouped_words.rearrange(
             "p (g t j u) -> p g t j u", g=POS_PASSES, t=V_BLOCKS, u=2
         )
-        v_codes = keep.tile([P, POS_PASSES, V_BLOCKS, P], U32, align_bytes=64)
-        v_scales = keep.tile([P, POS_PASSES, V_BLOCKS, P], U8, align_bytes=64)
-
-        def transpose_v(t):
+        for t in range(V_BLOCKS):
             v_words_in = v_sb[:, t, :].bitcast(F32)
-            vT_ps = psum_two.tile([P, POS_PASSES * 2, P], F32, tag="bank")
+            vT_ps = psum_shared.tile([P, POS_PASSES * 2, P], F32, tag="bank")
             for g in range(POS_PASSES):
                 for u in range(2):
                     nc.tensor.transpose(
@@ -115,58 +110,55 @@ def tile_selfattentionconv2d_pb_t_kernel(
                 out=v_grouped_words[:, :, t, :, :],
                 in_=vT_ps[:].rearrange("p (g u) j -> p g j u", u=2),
             )
-
-        def quantise_v():
-            nc.vector.quantize_mx(
-                out=v_codes[:].rearrange("p g t j -> p (g t j)").bitcast(FP8X4),
-                scales=v_scales[:].rearrange("p g t j -> p (g t j)"),
-                in_=v_grouped[:].rearrange("p g t j k -> p (g t j k)"),
-            )
+        v_codes = keep.tile([P, POS_PASSES, V_BLOCKS, P], U32, align_bytes=64)
+        v_scales = keep.tile([P, POS_PASSES, V_BLOCKS, P], U8, align_bytes=64)
+        nc.vector.quantize_mx(
+            out=v_codes[:].rearrange("p g t j -> p (g t j)").bitcast(FP8X4),
+            scales=v_scales[:].rearrange("p g t j -> p (g t j)"),
+            in_=v_grouped[:].rearrange("p g t j k -> p (g t j k)"),
+        )
 
         score_banks = {}
-        half_maxima = {}
         neg_max = {}
         e_rows = {}
         e_sums = {}
         e_banks = {}
         e_grouped = {}
         e_packed = {}
-        inverses = {}
-        inv_banks = {}
-        inv_spread = {}
+        inv_sum = {}
         att_banks = {}
         att_grouped = {}
         att_packed = {}
         y_banks = {}
 
-        def scores(i, h):
-            s_ps = psum_scores.tile([P, BANK], F32, name="s_ps%d" % h)
-            nc.tensor.matmul(
-                out=s_ps[:],
-                lhsT=q_sb[:, P * i : P * (i + 1)],
-                rhs=k_sorted[:, BANK * h : BANK * (h + 1)],
-                start=True,
-                stop=True,
-            )
-            score_banks[(i, h)] = s_ps
-
-        def half_max(i):
-            maxima = small.tile([P, POS_HALVES], F32)
+        def scores(i):
+            halves = []
             for h in range(POS_HALVES):
-                nc.vector.reduce_max(out=maxima[:, h : h + 1], in_=score_banks[(i, h)][:], axis=AXIS_X)
-            half_maxima[i] = maxima
+                s_ps = psum_scores.tile([P, BANK], F32, name="s_ps%d" % h)
+                nc.tensor.matmul(
+                    out=s_ps[:],
+                    lhsT=q_sb[:, P * i : P * (i + 1)],
+                    rhs=k_sorted[:, BANK * h : BANK * (h + 1)],
+                    start=True,
+                    stop=True,
+                )
+                halves.append(s_ps)
+            score_banks[i] = halves
 
-        def minus_max(i):
-            negated = small.tile([P, 1], F32)
+        def row_max(i):
+            half_max = small.tile([P, POS_HALVES], F32)
+            for h in range(POS_HALVES):
+                nc.vector.reduce_max(out=half_max[:, h : h + 1], in_=score_banks[i][h][:], axis=AXIS_X)
+            minus_max = small.tile([P, 1], F32)
             nc.vector.tensor_scalar(
-                out=negated[:],
-                in0=half_maxima[i][:, 0:1],
-                scalar1=half_maxima[i][:, 1:2],
+                out=minus_max[:],
+                in0=half_max[:, 0:1],
+                scalar1=half_max[:, 1:2],
                 scalar2=-1.0,
                 op0=ALU.max,
                 op1=ALU.mult,
             )
-            neg_max[i] = negated
+            neg_max[i] = minus_max
 
         def exponentials(i):
             group, member = divmod(i, GROUP)
@@ -176,7 +168,7 @@ def tile_selfattentionconv2d_pb_t_kernel(
             for h in range(POS_HALVES):
                 nc.scalar.activation(
                     out=e_bf[:, BANK * h : BANK * (h + 1)],
-                    in_=score_banks[(i, h)][:],
+                    in_=score_banks[i][h][:],
                     func=ACT.Exp,
                     bias=neg_max[i][:, 0:1],
                     scale=1.0,
@@ -185,7 +177,7 @@ def tile_selfattentionconv2d_pb_t_kernel(
             e_rows[i] = e_bf
 
         def transpose_e(i):
-            eT_ps = psum_one.tile([P, POS_PASSES * 2, P], F32)
+            eT_ps = psum_shared.tile([P, POS_PASSES * 2, P], F32, tag="bank")
             words = e_rows[i][:].bitcast(F32)
             for b in range(POS_PASSES * 2):
                 nc.tensor.transpose(eT_ps[:, b, :], words[:, P * b : P * (b + 1)], ident[:])
@@ -209,31 +201,23 @@ def tile_selfattentionconv2d_pb_t_kernel(
             )
             e_packed[i] = (e_codes, e_scales)
 
-        def invert_row_sums(group):
+        def spread_row_sums(group):
             row_sum = small.tile([P, GROUP], F32)
             nc.vector.reduce_sum(out=row_sum[:], in_=e_sums[group][:], axis=AXIS_X)
             inverse = small.tile([P, GROUP], F32)
             nc.vector.reciprocal(out=inverse[:], in_=row_sum[:])
-            inverses[group] = inverse
-
-        def transpose_inverses(group):
-            inv_ps = psum_two.tile([P, GROUP, P], F32, tag="bank")
+            inv_ps = psum_shared.tile([P, GROUP, P], F32, tag="bank")
             for member in range(GROUP):
                 nc.tensor.transpose(
-                    inv_ps[:, member, :],
-                    inverses[group][:, member : member + 1].to_broadcast([P, P]),
-                    ident[:],
+                    inv_ps[:, member, :], inverse[:, member : member + 1].to_broadcast([P, P]), ident[:]
                 )
-            inv_banks[group] = inv_ps
-
-        def copy_inverses(group):
             inv_sb = stream.tile([P, GROUP, P], F32)
-            nc.scalar.copy(out=inv_sb[:], in_=inv_banks[group][:])
-            inv_spread[group] = inv_sb
+            nc.scalar.copy(out=inv_sb[:], in_=inv_ps[:])
+            inv_sum[group] = inv_sb
 
         def attend(i):
             e_codes, e_scales = e_packed[i]
-            att_ps = psum_one.tile([P, V_BLOCKS, P], F32)
+            att_ps = psum_shared.tile([P, V_BLOCKS, P], F32, tag="bank")
             for t in range(V_BLOCKS):
                 for g in range(POS_PASSES):
                     nc.tensor.matmul_mx(
@@ -254,13 +238,13 @@ def tile_selfattentionconv2d_pb_t_kernel(
             nc.vector.tensor_tensor(
                 out=att_grouped[group][:, member, :, :],
                 in0=att_banks[i][:].rearrange("p t n -> p n t"),
-                in1=inv_spread[group][:, member, :].unsqueeze(2).to_broadcast([P, P, PACK]),
+                in1=inv_sum[group][:, member, :].unsqueeze(2).to_broadcast([P, P, PACK]),
                 op=ALU.mult,
             )
 
         def quantise_att(group):
-            att_codes = stream.tile([P, GROUP_PIX], U32, align_bytes=64)
-            att_scales = stream.tile([P, GROUP_PIX], U8, align_bytes=64)
+            att_codes = stream.tile([P, GROUP * P], U32, align_bytes=64)
+            att_scales = stream.tile([P, GROUP * P], U8, align_bytes=64)
             nc.vector.quantize_mx(
                 out=att_codes[:].bitcast(FP8X4),
                 scales=att_scales[:],
@@ -268,79 +252,63 @@ def tile_selfattentionconv2d_pb_t_kernel(
             )
             att_packed[group] = (att_codes, att_scales)
 
-        def project(group, unit):
+        def project(group, cb):
             att_codes, att_scales = att_packed[group]
-            y_ps = psum_two.tile([P, UNIT_BLOCKS, GROUP_PIX], F32, tag="bank")
-            for b in range(UNIT_BLOCKS):
-                cb = UNIT_BLOCKS * unit + b
-                nc.tensor.matmul_mx(
-                    out=y_ps[:, b, :],
-                    lhsT=w_words[:, P * PACK * cb : P * PACK * (cb + 1)].bitcast(FP8X4),
-                    lhsT_scale=w_scales[:, P * cb : P * (cb + 1)],
-                    rhs=att_codes[:].bitcast(FP8X4),
-                    rhs_scale=att_scales[:],
-                    start=True,
-                    stop=True,
-                )
-            y_banks[(group, unit)] = y_ps
+            y_ps = psum_shared.tile([P, GROUP * P], F32, tag="bank")
+            nc.tensor.matmul_mx(
+                out=y_ps[:],
+                lhsT=w_words[:, P * PACK * cb : P * PACK * (cb + 1)].bitcast(FP8X4),
+                lhsT_scale=w_scales[:, P * cb : P * (cb + 1)],
+                rhs=att_codes[:].bitcast(FP8X4),
+                rhs_scale=att_scales[:],
+                start=True,
+                stop=True,
+            )
+            y_banks[(group, cb)] = y_ps
 
-        def residual(group, unit):
-            blocks = slice(UNIT_BLOCKS * unit, UNIT_BLOCKS * (unit + 1))
-            pixels = slice(GROUP_PIX * group, GROUP_PIX * (group + 1))
-            o_sb = results.tile([P, UNIT_BLOCKS, GROUP_PIX], F32)
-            if group == N_TILES // GROUP - 1:
+        def residual(group, cb):
+            pixels = slice(GROUP * P * group, GROUP * P * (group + 1))
+            o_sb = results.tile([P, GROUP * P], F32)
+            if cb == 0 or group == N_GROUPS - 1:
                 nc.vector.scalar_tensor_tensor(
                     out=o_sb[:],
-                    in0=y_banks[(group, unit)][:],
+                    in0=y_banks[(group, cb)][:],
                     scalar=gain_f32[:, 0:1],
-                    in1=imgs_sb[:, blocks, pixels],
+                    in1=imgs_sb[:, cb, pixels],
                     op0=ALU.mult,
                     op1=ALU.add,
                 )
             else:
                 nc.scalar.activation(
-                    out=o_sb[:], in_=y_banks[(group, unit)][:], func=ACT.Copy, scale=gain_f32[:, 0:1]
+                    out=o_sb[:], in_=y_banks[(group, cb)][:], func=ACT.Copy, scale=gain_f32[:, 0:1]
                 )
-                nc.gpsimd.tensor_tensor(out=o_sb[:], in0=o_sb[:], in1=imgs_sb[:, blocks, pixels], op=ALU.add)
-            nc.sync.dma_start(out=out_rows[:, blocks, pixels], in_=o_sb[:])
+                nc.gpsimd.tensor_tensor(out=o_sb[:], in0=o_sb[:], in1=imgs_sb[:, cb, pixels], op=ALU.add)
+            nc.sync.dma_start(out=out_rows[:, cb, pixels], in_=o_sb[:])
 
         def is_tile(i):
             return 0 <= i < N_TILES
 
-        def closes_group(i):
-            return is_tile(i) and i % GROUP == GROUP - 1
-
-        for step in range(-1, N_TILES + 5):
-            if closes_group(step - 2):
-                invert_row_sums((step - 2) // GROUP)
-                transpose_inverses((step - 2) // GROUP)
-            if is_tile(step - 5):
-                project((step - 5) // GROUP, (step - 5) % GROUP)
-            if is_tile(step - 3):
-                attend(step - 3)
+        for step in range(-1, N_TILES + ATTEND_LAG + GROUP):
+            if is_tile(step - ATTEND_LAG):
+                attend(step - ATTEND_LAG)
+            group, cb = divmod(step - ATTEND_LAG - GROUP, GROUP)
+            if 0 <= group < N_GROUPS:
+                project(group, cb)
             if is_tile(step + 1):
-                scores(step + 1, 0)
-                scores(step + 1, 1)
+                scores(step + 1)
+            if is_tile(step):
+                row_max(step)
             if is_tile(step - 1):
                 exponentials(step - 1)
                 transpose_e(step - 1)
-            if is_tile(step - 2):
-                regroup_e(step - 2)
-            if closes_group(step - 2):
-                copy_inverses((step - 2) // GROUP)
-            if is_tile(step):
-                half_max(step)
-                minus_max(step)
+                regroup_e(step - 1)
+            if is_tile(step - ATTEND_LAG):
+                normalise(step - ATTEND_LAG)
             if is_tile(step - 2):
                 quantise_e(step - 2)
-            if is_tile(step - 5):
-                residual((step - 5) // GROUP, (step - 5) % GROUP)
-            if is_tile(step - 3):
-                normalise(step - 3)
-            if closes_group(step - 3):
-                quantise_att((step - 3) // GROUP)
-            if step in (1, 2):
-                for t in range(V_ROUNDS_A_STEP * (step - 1), V_ROUNDS_A_STEP * step):
-                    transpose_v(t)
-            if step == 2:
-                quantise_v()
+            if is_tile(step - 1) and (step - 1) % GROUP == GROUP - 1:
+                spread_row_sums((step - 1) // GROUP)
+            if is_tile(step - ATTEND_LAG) and (step - ATTEND_LAG) % GROUP == GROUP - 1:
+                quantise_att((step - ATTEND_LAG) // GROUP)
+            if 0 <= group < N_GROUPS:
+                residual(group, cb)

@@ -32,7 +32,7 @@ POS_HALVES = N_POS // BANK
 V_BLOCKS = D_V // P
 C_BLOCKS = C_OUT // P
 
-ATTEND_LAG = 5
+PAIR = 2
 
 FLOPS = 2 * N_PIX * N_POS * D_QK + 2 * N_PIX * N_POS * D_V + 2 * N_PIX * D_V * C_OUT
 
@@ -45,7 +45,7 @@ def tile_selfattentionconv2d_pb_t_kernel(
         keep = stack.enter_context(tc.tile_pool(name="keep", bufs=1))
         small = stack.enter_context(tc.tile_pool(name="small", bufs=4))
         stream = stack.enter_context(tc.tile_pool(name="stream", bufs=3))
-        packed = stack.enter_context(tc.tile_pool(name="packed", bufs=ATTEND_LAG + 2))
+        packed = stack.enter_context(tc.tile_pool(name="packed", bufs=4))
         results = stack.enter_context(tc.tile_pool(name="results", bufs=4))
         psum_scores = stack.enter_context(tc.psum_pool(name="psum_scores", bufs=2))
         psum_shared = stack.enter_context(tc.psum_pool(name="psum_shared", bufs=4))
@@ -56,8 +56,8 @@ def tile_selfattentionconv2d_pb_t_kernel(
         q_rows = q.rearrange("b d n -> (b d) n")
         first = GROUP * P
         nc.sync.dma_start(out=q_sb[:, :first], in_=q_rows[:, :first])
-        v_sb = keep.tile([P, PACK, N_POS], BF16)
-        nc.sync.dma_start(out=v_sb[:], in_=v_pool.rearrange("b (j t) m -> (b j) t m", t=PACK))
+        v_sb = keep.tile([P, V_BLOCKS, N_POS], BF16)
+        nc.sync.dma_start(out=v_sb[:], in_=v_pool.rearrange("b (t j) m -> j (b t) m", j=P))
         nc.sync.dma_start(out=q_sb[:, first:], in_=q_rows[:, first:])
         gain_bf = keep.tile([P, 1], BF16)
         nc.sync.dma_start(out=gain_bf[:], in_=gain.partition_broadcast(P))
@@ -127,6 +127,8 @@ def tile_selfattentionconv2d_pb_t_kernel(
         e_packed = {}
         inv_sum = {}
         att_banks = {}
+        att_rows = {}
+        attT_banks = {}
         att_grouped = {}
         att_packed = {}
         y_banks = {}
@@ -161,9 +163,9 @@ def tile_selfattentionconv2d_pb_t_kernel(
             neg_max[i] = minus_max
 
         def exponentials(i):
-            group, member = divmod(i, GROUP)
+            pair, member = divmod(i, PAIR)
             if member == 0:
-                e_sums[group] = small.tile([P, GROUP, POS_HALVES], F32, name="sums")
+                e_sums[pair] = small.tile([P, PAIR, POS_HALVES], F32, name="sums")
             e_bf = stream.tile([P, N_POS], BF16)
             for h in range(POS_HALVES):
                 nc.scalar.activation(
@@ -172,7 +174,7 @@ def tile_selfattentionconv2d_pb_t_kernel(
                     func=ACT.Exp,
                     bias=neg_max[i][:, 0:1],
                     scale=1.0,
-                    accum_out=e_sums[group][:, member, h : h + 1],
+                    accum_out=e_sums[pair][:, member, h : h + 1],
                 )
             e_rows[i] = e_bf
 
@@ -201,45 +203,56 @@ def tile_selfattentionconv2d_pb_t_kernel(
             )
             e_packed[i] = (e_codes, e_scales)
 
-        def spread_row_sums(group):
-            row_sum = small.tile([P, GROUP], F32)
-            nc.vector.reduce_sum(out=row_sum[:], in_=e_sums[group][:], axis=AXIS_X)
-            inverse = small.tile([P, GROUP], F32)
+        def invert_row_sums(pair):
+            row_sum = small.tile([P, PAIR], F32)
+            nc.vector.reduce_sum(out=row_sum[:], in_=e_sums[pair][:], axis=AXIS_X)
+            inverse = small.tile([P, PAIR], F32)
             nc.vector.reciprocal(out=inverse[:], in_=row_sum[:])
-            inv_ps = psum_shared.tile([P, GROUP, P], F32, tag="bank")
-            for member in range(GROUP):
-                nc.tensor.transpose(
-                    inv_ps[:, member, :], inverse[:, member : member + 1].to_broadcast([P, P]), ident[:]
-                )
-            inv_sb = stream.tile([P, GROUP, P], F32)
-            nc.scalar.copy(out=inv_sb[:], in_=inv_ps[:])
-            inv_sum[group] = inv_sb
+            inv_sum[pair] = inverse
 
         def attend(i):
             e_codes, e_scales = e_packed[i]
-            att_ps = psum_shared.tile([P, V_BLOCKS, P], F32, tag="bank")
-            for t in range(V_BLOCKS):
-                for g in range(POS_PASSES):
-                    nc.tensor.matmul_mx(
-                        out=att_ps[:, t, :],
-                        lhsT=v_codes[:, g, t, :].bitcast(FP8X4),
-                        lhsT_scale=v_scales[:, g, t, :],
-                        rhs=e_codes[:, g, :].bitcast(FP8X4),
-                        rhs_scale=e_scales[:, g, :],
-                        start=(g == 0),
-                        stop=(g == POS_PASSES - 1),
-                    )
+            att_ps = psum_shared.tile([P, D_V], F32, tag="bank")
+            for g in range(POS_PASSES):
+                nc.tensor.matmul_mx(
+                    out=att_ps[:],
+                    lhsT=e_codes[:, g, :].bitcast(FP8X4),
+                    lhsT_scale=e_scales[:, g, :],
+                    rhs=v_codes[:, g, :, :].rearrange("p t j -> p (t j)").bitcast(FP8X4),
+                    rhs_scale=v_scales[:, g, :, :].rearrange("p t j -> p (t j)"),
+                    start=(g == 0),
+                    stop=(g == POS_PASSES - 1),
+                )
             att_banks[i] = att_ps
 
         def normalise(i):
-            group, member = divmod(i, GROUP)
-            if member == 0:
-                att_grouped[group] = stream.tile([P, GROUP, P, PACK], BF16, name="att_grp", align_bytes=64)
-            nc.vector.tensor_tensor(
-                out=att_grouped[group][:, member, :, :],
-                in0=att_banks[i][:].rearrange("p t n -> p n t"),
-                in1=inv_sum[group][:, member, :].unsqueeze(2).to_broadcast([P, P, PACK]),
-                op=ALU.mult,
+            pair, member = divmod(i, PAIR)
+            att_bf = stream.tile([P, D_V], BF16)
+            nc.scalar.activation(
+                out=att_bf[:].rearrange("n (u p e) -> n u p e", u=2, e=2),
+                in_=att_banks[i][:].rearrange("n (p u e) -> n u p e", u=2, e=2),
+                func=ACT.Copy,
+                scale=inv_sum[pair][:, member : member + 1],
+            )
+            att_rows[i] = att_bf
+
+        def transpose_att(pair):
+            attT_ps = psum_shared.tile([P, PAIR, 2, P], F32, tag="bank")
+            for member in range(PAIR):
+                words = att_rows[PAIR * pair + member][:].bitcast(F32)
+                for u in range(2):
+                    nc.tensor.transpose(attT_ps[:, member, u, :], words[:, P * u : P * (u + 1)], ident[:])
+            attT_banks[pair] = attT_ps
+
+        def regroup_att(pair):
+            group, half = divmod(pair, GROUP // PAIR)
+            if half == 0:
+                att_grouped[group] = stream.tile([P, GROUP * P * PACK], BF16, name="att_grp", align_bytes=64)
+            words = att_grouped[group][:].bitcast(F32).rearrange("p (m n u) -> p m n u", m=GROUP, u=2)
+            engine_copy = nc.scalar.copy if half == 0 else nc.vector.tensor_copy
+            engine_copy(
+                out=words[:, PAIR * half : PAIR * (half + 1), :, :],
+                in_=attT_banks[pair][:].rearrange("p m u n -> p m n u"),
             )
 
         def quantise_att(group):
@@ -248,7 +261,7 @@ def tile_selfattentionconv2d_pb_t_kernel(
             nc.vector.quantize_mx(
                 out=att_codes[:].bitcast(FP8X4),
                 scales=att_scales[:],
-                in_=att_grouped[group][:].rearrange("p m n t -> p (m n t)"),
+                in_=att_grouped[group][:],
             )
             att_packed[group] = (att_codes, att_scales)
 
@@ -269,29 +282,23 @@ def tile_selfattentionconv2d_pb_t_kernel(
         def residual(group, cb):
             pixels = slice(GROUP * P * group, GROUP * P * (group + 1))
             o_sb = results.tile([P, GROUP * P], F32)
-            if cb == 0 or group == N_GROUPS - 1:
-                nc.vector.scalar_tensor_tensor(
-                    out=o_sb[:],
-                    in0=y_banks[(group, cb)][:],
-                    scalar=gain_f32[:, 0:1],
-                    in1=imgs_sb[:, cb, pixels],
-                    op0=ALU.mult,
-                    op1=ALU.add,
-                )
-            else:
-                nc.scalar.activation(
-                    out=o_sb[:], in_=y_banks[(group, cb)][:], func=ACT.Copy, scale=gain_f32[:, 0:1]
-                )
-                nc.gpsimd.tensor_tensor(out=o_sb[:], in0=o_sb[:], in1=imgs_sb[:, cb, pixels], op=ALU.add)
+            nc.vector.scalar_tensor_tensor(
+                out=o_sb[:],
+                in0=y_banks[(group, cb)][:],
+                scalar=gain_f32[:, 0:1],
+                in1=imgs_sb[:, cb, pixels],
+                op0=ALU.mult,
+                op1=ALU.add,
+            )
             nc.sync.dma_start(out=out_rows[:, cb, pixels], in_=o_sb[:])
 
         def is_tile(i):
             return 0 <= i < N_TILES
 
-        for step in range(-1, N_TILES + ATTEND_LAG + GROUP):
-            if is_tile(step - ATTEND_LAG):
-                attend(step - ATTEND_LAG)
-            group, cb = divmod(step - ATTEND_LAG - GROUP, GROUP)
+        for step in range(-1, N_TILES + 9 + GROUP):
+            if is_tile(step - 3):
+                attend(step - 3)
+            group, cb = divmod(step - 9, GROUP)
             if 0 <= group < N_GROUPS:
                 project(group, cb)
             if is_tile(step + 1):
@@ -301,14 +308,19 @@ def tile_selfattentionconv2d_pb_t_kernel(
             if is_tile(step - 1):
                 exponentials(step - 1)
                 transpose_e(step - 1)
+            if is_tile(step - 4) and (step - 4) % PAIR == PAIR - 1:
+                transpose_att((step - 4) // PAIR)
+            if is_tile(step - 1):
                 regroup_e(step - 1)
-            if is_tile(step - ATTEND_LAG):
-                normalise(step - ATTEND_LAG)
+            if is_tile(step - 3):
+                normalise(step - 3)
             if is_tile(step - 2):
                 quantise_e(step - 2)
-            if is_tile(step - 1) and (step - 1) % GROUP == GROUP - 1:
-                spread_row_sums((step - 1) // GROUP)
-            if is_tile(step - ATTEND_LAG) and (step - ATTEND_LAG) % GROUP == GROUP - 1:
-                quantise_att((step - ATTEND_LAG) // GROUP)
+            if is_tile(step - 1) and (step - 1) % PAIR == PAIR - 1:
+                invert_row_sums((step - 1) // PAIR)
+            if is_tile(step - 4) and (step - 4) % PAIR == PAIR - 1:
+                regroup_att((step - 4) // PAIR)
+            if is_tile(step - 5) and (step - 5) % GROUP == GROUP - 1:
+                quantise_att((step - 5) // GROUP)
             if 0 <= group < N_GROUPS:
                 residual(group, cb)

@@ -33,6 +33,8 @@ V_BLOCKS = D_V // P
 C_BLOCKS = C_OUT // P
 
 PAIR = 2
+TAIL_BLOCKS = 9
+ROLES = ("eT", "att", "attT", "y")
 
 FLOPS = 2 * N_PIX * N_POS * D_QK + 2 * N_PIX * N_POS * D_V + 2 * N_PIX * D_V * C_OUT
 
@@ -46,9 +48,9 @@ def tile_selfattentionconv2d_pb_t_kernel(
         small = stack.enter_context(tc.tile_pool(name="small", bufs=4))
         stream = stack.enter_context(tc.tile_pool(name="stream", bufs=3))
         packed = stack.enter_context(tc.tile_pool(name="packed", bufs=4))
-        results = stack.enter_context(tc.tile_pool(name="results", bufs=4))
+        results = stack.enter_context(tc.tile_pool(name="results", bufs=8))
         psum_scores = stack.enter_context(tc.psum_pool(name="psum_scores", bufs=2))
-        psum_shared = stack.enter_context(tc.psum_pool(name="psum_shared", bufs=4))
+        psum_roles = stack.enter_context(tc.psum_pool(name="psum_roles", bufs=1))
 
         k_sb = keep.tile([P, N_POS], BF16)
         nc.sync.dma_start(out=k_sb[:], in_=k_pool.rearrange("b d m -> (b d) m"))
@@ -83,7 +85,6 @@ def tile_selfattentionconv2d_pb_t_kernel(
         ident = keep.tile([P, P], F32)
         make_identity(nc, ident[:])
         gain_f32 = keep.tile([P, 1], F32)
-        nc.vector.tensor_copy(out=gain_f32[:], in_=gain_bf[:])
 
         k_sorted = keep.tile([P, N_POS], BF16)
         nc.vector.tensor_copy(
@@ -96,9 +97,13 @@ def tile_selfattentionconv2d_pb_t_kernel(
         v_grouped_words = v_grouped_words.rearrange(
             "p (g t j u) -> p g t j u", g=POS_PASSES, t=V_BLOCKS, u=2
         )
-        for t in range(V_BLOCKS):
+        v_banks = {}
+        v_codes = keep.tile([P, POS_PASSES, V_BLOCKS, P], U32, align_bytes=64)
+        v_scales = keep.tile([P, POS_PASSES, V_BLOCKS, P], U8, align_bytes=64)
+
+        def transpose_v(t):
             v_words_in = v_sb[:, t, :].bitcast(F32)
-            vT_ps = psum_shared.tile([P, POS_PASSES * 2, P], F32, tag="bank")
+            vT_ps = psum_roles.tile([P, POS_PASSES * 2, P], F32, tag=ROLES[t])
             for g in range(POS_PASSES):
                 for u in range(2):
                     nc.tensor.transpose(
@@ -106,20 +111,25 @@ def tile_selfattentionconv2d_pb_t_kernel(
                         v_words_in[:, 256 * g + u : 256 * (g + 1) : 2],
                         ident[:],
                     )
+            v_banks[t] = vT_ps
+
+        def regroup_v(t):
             nc.vector.tensor_copy(
                 out=v_grouped_words[:, :, t, :, :],
-                in_=vT_ps[:].rearrange("p (g u) j -> p g j u", u=2),
+                in_=v_banks[t][:].rearrange("p (g u) j -> p g j u", u=2),
             )
-        v_codes = keep.tile([P, POS_PASSES, V_BLOCKS, P], U32, align_bytes=64)
-        v_scales = keep.tile([P, POS_PASSES, V_BLOCKS, P], U8, align_bytes=64)
-        nc.vector.quantize_mx(
-            out=v_codes[:].rearrange("p g t j -> p (g t j)").bitcast(FP8X4),
-            scales=v_scales[:].rearrange("p g t j -> p (g t j)"),
-            in_=v_grouped[:].rearrange("p g t j k -> p (g t j k)"),
-        )
+
+        def quantise_v():
+            nc.vector.quantize_mx(
+                out=v_codes[:].rearrange("p g t j -> p (g t j)").bitcast(FP8X4),
+                scales=v_scales[:].rearrange("p g t j -> p (g t j)"),
+                in_=v_grouped[:].rearrange("p g t j k -> p (g t j k)"),
+            )
 
         score_banks = {}
+        half_maxes = {}
         neg_max = {}
+        row_sums = {}
         e_rows = {}
         e_sums = {}
         e_banks = {}
@@ -147,10 +157,14 @@ def tile_selfattentionconv2d_pb_t_kernel(
                 halves.append(s_ps)
             score_banks[i] = halves
 
-        def row_max(i):
+        def half_maxima(i):
             half_max = small.tile([P, POS_HALVES], F32)
             for h in range(POS_HALVES):
                 nc.vector.reduce_max(out=half_max[:, h : h + 1], in_=score_banks[i][h][:], axis=AXIS_X)
+            half_maxes[i] = half_max
+
+        def row_max(i):
+            half_max = half_maxes[i]
             minus_max = small.tile([P, 1], F32)
             nc.vector.tensor_scalar(
                 out=minus_max[:],
@@ -179,7 +193,7 @@ def tile_selfattentionconv2d_pb_t_kernel(
             e_rows[i] = e_bf
 
         def transpose_e(i):
-            eT_ps = psum_shared.tile([P, POS_PASSES * 2, P], F32, tag="bank")
+            eT_ps = psum_roles.tile([P, POS_PASSES * 2, P], F32, tag="eT")
             words = e_rows[i][:].bitcast(F32)
             for b in range(POS_PASSES * 2):
                 nc.tensor.transpose(eT_ps[:, b, :], words[:, P * b : P * (b + 1)], ident[:])
@@ -187,7 +201,8 @@ def tile_selfattentionconv2d_pb_t_kernel(
 
         def regroup_e(i):
             e_grp = stream.tile([P, POS_PASSES * P * PACK], BF16, align_bytes=64)
-            nc.scalar.copy(
+            engine_copy = nc.vector.tensor_copy if 2 <= i < 6 else nc.scalar.copy
+            engine_copy(
                 out=e_grp[:].bitcast(F32).rearrange("p (g n u) -> p g n u", g=POS_PASSES, u=2),
                 in_=e_banks[i][:].rearrange("p (g u) n -> p g n u", u=2),
             )
@@ -203,16 +218,19 @@ def tile_selfattentionconv2d_pb_t_kernel(
             )
             e_packed[i] = (e_codes, e_scales)
 
-        def invert_row_sums(pair):
+        def add_row_sums(pair):
             row_sum = small.tile([P, PAIR], F32)
             nc.vector.reduce_sum(out=row_sum[:], in_=e_sums[pair][:], axis=AXIS_X)
+            row_sums[pair] = row_sum
+
+        def invert_row_sums(pair):
             inverse = small.tile([P, PAIR], F32)
-            nc.vector.reciprocal(out=inverse[:], in_=row_sum[:])
+            nc.vector.reciprocal(out=inverse[:], in_=row_sums[pair][:])
             inv_sum[pair] = inverse
 
         def attend(i):
             e_codes, e_scales = e_packed[i]
-            att_ps = psum_shared.tile([P, D_V], F32, tag="bank")
+            att_ps = psum_roles.tile([P, D_V], F32, tag="att")
             for g in range(POS_PASSES):
                 nc.tensor.matmul_mx(
                     out=att_ps[:],
@@ -237,7 +255,7 @@ def tile_selfattentionconv2d_pb_t_kernel(
             att_rows[i] = att_bf
 
         def transpose_att(pair):
-            attT_ps = psum_shared.tile([P, PAIR, 2, P], F32, tag="bank")
+            attT_ps = psum_roles.tile([P, PAIR, 2, P], F32, tag="attT")
             for member in range(PAIR):
                 words = att_rows[PAIR * pair + member][:].bitcast(F32)
                 for u in range(2):
@@ -249,7 +267,7 @@ def tile_selfattentionconv2d_pb_t_kernel(
             if half == 0:
                 att_grouped[group] = stream.tile([P, GROUP * P * PACK], BF16, name="att_grp", align_bytes=64)
             words = att_grouped[group][:].bitcast(F32).rearrange("p (m n u) -> p m n u", m=GROUP, u=2)
-            engine_copy = nc.scalar.copy if half == 0 else nc.vector.tensor_copy
+            engine_copy = nc.scalar.copy if pair == 15 or pair % 4 == 0 else nc.vector.tensor_copy
             engine_copy(
                 out=words[:, PAIR * half : PAIR * (half + 1), :, :],
                 in_=attT_banks[pair][:].rearrange("p m u n -> p m n u"),
@@ -267,7 +285,10 @@ def tile_selfattentionconv2d_pb_t_kernel(
 
         def project(group, cb):
             att_codes, att_scales = att_packed[group]
-            y_ps = psum_shared.tile([P, GROUP * P], F32, tag="bank")
+            if GROUP * group + cb < N_TILES - TAIL_BLOCKS:
+                y_ps = psum_roles.tile([P, GROUP * P], F32, tag="y")
+            else:
+                y_ps = psum_scores.tile([P, GROUP * P], F32, name="s_ps%d" % (cb % POS_HALVES))
             nc.tensor.matmul_mx(
                 out=y_ps[:],
                 lhsT=w_words[:, P * PACK * cb : P * PACK * (cb + 1)].bitcast(FP8X4),
@@ -295,32 +316,52 @@ def tile_selfattentionconv2d_pb_t_kernel(
         def is_tile(i):
             return 0 <= i < N_TILES
 
-        for step in range(-1, N_TILES + 9 + GROUP):
-            if is_tile(step - 3):
-                attend(step - 3)
+        def is_last_of(i, count):
+            return is_tile(i) and i % count == count - 1
+
+        stack.enter_context(tc.manual_schedule())
+        for step in range(-2, N_TILES + 9 + GROUP):
             group, cb = divmod(step - 9, GROUP)
-            if 0 <= group < N_GROUPS:
-                project(group, cb)
-            if is_tile(step + 1):
-                scores(step + 1)
+            has_block = 0 <= group < N_GROUPS
             if is_tile(step):
-                row_max(step)
+                exponentials(step)
             if is_tile(step - 1):
-                exponentials(step - 1)
                 transpose_e(step - 1)
-            if is_tile(step - 4) and (step - 4) % PAIR == PAIR - 1:
-                transpose_att((step - 4) // PAIR)
+            if has_block:
+                project(group, cb)
+            if is_tile(step - 2):
+                attend(step - 2)
+            if is_last_of(step - 3, PAIR):
+                transpose_att((step - 3) // PAIR)
+            if is_tile(step + 2):
+                scores(step + 2)
+            if step in (-1, 0):
+                transpose_v(2 * step + 2)
+                transpose_v(2 * step + 3)
+            if is_tile(step + 1):
+                half_maxima(step + 1)
+            if has_block:
+                residual(group, cb)
+            if is_tile(step + 1):
+                row_max(step + 1)
+            if step in (0, 1):
+                regroup_v(2 * step)
+                regroup_v(2 * step + 1)
             if is_tile(step - 1):
                 regroup_e(step - 1)
-            if is_tile(step - 3):
-                normalise(step - 3)
             if is_tile(step - 2):
-                quantise_e(step - 2)
-            if is_tile(step - 1) and (step - 1) % PAIR == PAIR - 1:
-                invert_row_sums((step - 1) // PAIR)
-            if is_tile(step - 4) and (step - 4) % PAIR == PAIR - 1:
+                normalise(step - 2)
+            if is_last_of(step, PAIR):
+                add_row_sums(step // PAIR)
+            if is_last_of(step - 4, PAIR):
                 regroup_att((step - 4) // PAIR)
-            if is_tile(step - 5) and (step - 5) % GROUP == GROUP - 1:
+            if is_last_of(step, PAIR):
+                invert_row_sums(step // PAIR)
+            if is_last_of(step - 5, GROUP):
                 quantise_att((step - 5) // GROUP)
-            if 0 <= group < N_GROUPS:
-                residual(group, cb)
+            if step == 1:
+                quantise_v()
+            if step == 5:
+                nc.vector.tensor_copy(out=gain_f32[:], in_=gain_bf[:])
+            if is_tile(step - 1):
+                quantise_e(step - 1)

@@ -33,7 +33,6 @@ V_BLOCKS = D_V // P
 C_BLOCKS = C_OUT // P
 
 PAIR = 2
-TAIL_BLOCKS = 9
 ROLES = ("eT", "att", "attT", "y")
 
 FLOPS = 2 * N_PIX * N_POS * D_QK + 2 * N_PIX * N_POS * D_V + 2 * N_PIX * D_V * C_OUT
@@ -98,6 +97,14 @@ def tile_selfattentionconv2d_pb_t_kernel(
             "p (g t j u) -> p g t j u", g=POS_PASSES, t=V_BLOCKS, u=2
         )
         v_banks = {}
+        late_banks = []
+
+        def product_bank(role, late):
+            if late:
+                late_banks.append(role)
+                return psum_scores.tile([P, BANK], F32, name="s_ps%d" % (len(late_banks) % POS_HALVES))
+            return psum_roles.tile([P, BANK], F32, name=role)
+
         v_codes = keep.tile([P, POS_PASSES, V_BLOCKS, P], U32, align_bytes=64)
         v_scales = keep.tile([P, POS_PASSES, V_BLOCKS, P], U8, align_bytes=64)
 
@@ -114,7 +121,8 @@ def tile_selfattentionconv2d_pb_t_kernel(
             v_banks[t] = vT_ps
 
         def regroup_v(t):
-            nc.vector.tensor_copy(
+            engine_copy = nc.scalar.copy if t < 0 else nc.vector.tensor_copy
+            engine_copy(
                 out=v_grouped_words[:, :, t, :, :],
                 in_=v_banks[t][:].rearrange("p (g u) j -> p g j u", u=2),
             )
@@ -193,10 +201,10 @@ def tile_selfattentionconv2d_pb_t_kernel(
             e_rows[i] = e_bf
 
         def transpose_e(i):
-            eT_ps = psum_roles.tile([P, POS_PASSES * 2, P], F32, tag="eT")
+            eT_ps = product_bank("eT", i >= N_TILES - 1)
             words = e_rows[i][:].bitcast(F32)
             for b in range(POS_PASSES * 2):
-                nc.tensor.transpose(eT_ps[:, b, :], words[:, P * b : P * (b + 1)], ident[:])
+                nc.tensor.transpose(eT_ps[:, P * b : P * (b + 1)], words[:, P * b : P * (b + 1)], ident[:])
             e_banks[i] = eT_ps
 
         def regroup_e(i):
@@ -204,7 +212,7 @@ def tile_selfattentionconv2d_pb_t_kernel(
             engine_copy = nc.vector.tensor_copy if 2 <= i < 6 else nc.scalar.copy
             engine_copy(
                 out=e_grp[:].bitcast(F32).rearrange("p (g n u) -> p g n u", g=POS_PASSES, u=2),
-                in_=e_banks[i][:].rearrange("p (g u) n -> p g n u", u=2),
+                in_=e_banks[i][:].rearrange("p (g u n) -> p g n u", g=POS_PASSES, u=2),
             )
             e_grouped[i] = e_grp
 
@@ -230,7 +238,7 @@ def tile_selfattentionconv2d_pb_t_kernel(
 
         def attend(i):
             e_codes, e_scales = e_packed[i]
-            att_ps = psum_roles.tile([P, D_V], F32, tag="att")
+            att_ps = product_bank("att", i >= N_TILES - 2)
             for g in range(POS_PASSES):
                 nc.tensor.matmul_mx(
                     out=att_ps[:],
@@ -255,42 +263,43 @@ def tile_selfattentionconv2d_pb_t_kernel(
             att_rows[i] = att_bf
 
         def transpose_att(pair):
-            attT_ps = psum_roles.tile([P, PAIR, 2, P], F32, tag="attT")
+            attT_ps = product_bank("attT", False)
             for member in range(PAIR):
                 words = att_rows[PAIR * pair + member][:].bitcast(F32)
                 for u in range(2):
-                    nc.tensor.transpose(attT_ps[:, member, u, :], words[:, P * u : P * (u + 1)], ident[:])
+                    place = P * (2 * member + u)
+                    nc.tensor.transpose(attT_ps[:, place : place + P], words[:, P * u : P * (u + 1)], ident[:])
             attT_banks[pair] = attT_ps
 
         def regroup_att(pair):
-            group, half = divmod(pair, GROUP // PAIR)
-            if half == 0:
-                att_grouped[group] = stream.tile([P, GROUP * P * PACK], BF16, name="att_grp", align_bytes=64)
-            words = att_grouped[group][:].bitcast(F32).rearrange("p (m n u) -> p m n u", m=GROUP, u=2)
+            chunk, first_tile, tiles = chunk_of_tile[PAIR * pair]
+            place = PAIR * pair - first_tile
+            if place == 0:
+                att_grouped[chunk] = stream.tile([P, tiles * P * PACK], BF16, name="att_grp", align_bytes=64)
+            words = att_grouped[chunk][:].bitcast(F32).rearrange("p (m n u) -> p m n u", m=tiles, u=2)
             engine_copy = nc.scalar.copy if pair == 15 or pair % 4 == 0 else nc.vector.tensor_copy
             engine_copy(
-                out=words[:, PAIR * half : PAIR * (half + 1), :, :],
-                in_=attT_banks[pair][:].rearrange("p m u n -> p m n u"),
+                out=words[:, place : place + PAIR, :, :],
+                in_=attT_banks[pair][:].rearrange("p (m u n) -> p m n u", m=PAIR, u=2),
             )
 
-        def quantise_att(group):
-            att_codes = stream.tile([P, GROUP * P], U32, align_bytes=64)
-            att_scales = stream.tile([P, GROUP * P], U8, align_bytes=64)
+        def quantise_att(chunk):
+            tiles = chunks[chunk][1]
+            att_codes = stream.tile([P, tiles * P], U32, align_bytes=64)
+            att_scales = stream.tile([P, tiles * P], U8, align_bytes=64)
             nc.vector.quantize_mx(
                 out=att_codes[:].bitcast(FP8X4),
                 scales=att_scales[:],
-                in_=att_grouped[group][:],
+                in_=att_grouped[chunk][:],
             )
-            att_packed[group] = (att_codes, att_scales)
+            att_packed[chunk] = (att_codes, att_scales)
 
-        def project(group, cb):
-            att_codes, att_scales = att_packed[group]
-            if GROUP * group + cb < N_TILES - TAIL_BLOCKS:
-                y_ps = psum_roles.tile([P, GROUP * P], F32, tag="y")
-            else:
-                y_ps = psum_scores.tile([P, GROUP * P], F32, name="s_ps%d" % (cb % POS_HALVES))
+        def project(chunk, cb, late):
+            att_codes, att_scales = att_packed[chunk]
+            tiles = chunks[chunk][1]
+            y_ps = product_bank("y", late)
             nc.tensor.matmul_mx(
-                out=y_ps[:],
+                out=y_ps[:, : tiles * P],
                 lhsT=w_words[:, P * PACK * cb : P * PACK * (cb + 1)].bitcast(FP8X4),
                 lhsT_scale=w_scales[:, P * cb : P * (cb + 1)],
                 rhs=att_codes[:].bitcast(FP8X4),
@@ -298,14 +307,15 @@ def tile_selfattentionconv2d_pb_t_kernel(
                 start=True,
                 stop=True,
             )
-            y_banks[(group, cb)] = y_ps
+            y_banks[(chunk, cb)] = y_ps
 
-        def residual(group, cb):
-            pixels = slice(GROUP * P * group, GROUP * P * (group + 1))
-            o_sb = results.tile([P, GROUP * P], F32)
+        def residual(chunk, cb):
+            first_tile, tiles = chunks[chunk]
+            pixels = slice(P * first_tile, P * (first_tile + tiles))
+            o_sb = results.tile([P, tiles * P], F32)
             nc.vector.scalar_tensor_tensor(
                 out=o_sb[:],
-                in0=y_banks[(group, cb)][:],
+                in0=y_banks[(chunk, cb)][:, : tiles * P],
                 scalar=gain_f32[:, 0:1],
                 in1=imgs_sb[:, cb, pixels],
                 op0=ALU.mult,
@@ -319,34 +329,52 @@ def tile_selfattentionconv2d_pb_t_kernel(
         def is_last_of(i, count):
             return is_tile(i) and i % count == count - 1
 
+        chunks = [(GROUP * g, GROUP) for g in range(N_GROUPS - 1)]
+        chunks.extend([(N_TILES - GROUP + PAIR * h, PAIR) for h in range(GROUP // PAIR)])
+        chunk_of_tile = {}
+        for chunk, (first_tile, tiles) in enumerate(chunks):
+            for i in range(first_tile, first_tile + tiles):
+                chunk_of_tile[i] = (chunk, first_tile, tiles)
+        waiting = []
+        taken = 0
+
         stack.enter_context(tc.manual_schedule())
-        for step in range(-2, N_TILES + 9 + GROUP):
-            group, cb = divmod(step - 9, GROUP)
-            has_block = 0 <= group < N_GROUPS
+        for step in range(-2, N_TILES + 16):
+            late = step >= N_TILES
+            room = 2 * GROUP if late else GROUP
+            blocks = []
+            while taken < len(waiting) and chunks[waiting[taken][0]][1] <= room:
+                room -= chunks[waiting[taken][0]][1]
+                blocks.append(waiting[taken])
+                taken += 1
             if is_tile(step):
                 exponentials(step)
             if is_tile(step - 1):
                 transpose_e(step - 1)
-            if has_block:
-                project(group, cb)
+            for chunk, cb in blocks:
+                project(chunk, cb, late)
             if is_tile(step - 2):
                 attend(step - 2)
             if is_last_of(step - 3, PAIR):
                 transpose_att((step - 3) // PAIR)
             if is_tile(step + 2):
                 scores(step + 2)
-            if step in (-1, 0):
-                transpose_v(2 * step + 2)
-                transpose_v(2 * step + 3)
+            for t in range(V_BLOCKS):
+                if step == (t // 2) - 1:
+                    transpose_v(t)
+            for t in range(V_BLOCKS):
+                if step == t // 2 and t < 0:
+                    regroup_v(t)
             if is_tile(step + 1):
                 half_maxima(step + 1)
-            if has_block:
-                residual(group, cb)
+            if not late:
+                for chunk, cb in blocks:
+                    residual(chunk, cb)
             if is_tile(step + 1):
                 row_max(step + 1)
-            if step in (0, 1):
-                regroup_v(2 * step)
-                regroup_v(2 * step + 1)
+            for t in range(V_BLOCKS):
+                if step == t // 2 and t >= 0:
+                    regroup_v(t)
             if is_tile(step - 1):
                 regroup_e(step - 1)
             if is_tile(step - 2):
@@ -357,11 +385,15 @@ def tile_selfattentionconv2d_pb_t_kernel(
                 regroup_att((step - 4) // PAIR)
             if is_last_of(step, PAIR):
                 invert_row_sums(step // PAIR)
-            if is_last_of(step - 5, GROUP):
-                quantise_att((step - 5) // GROUP)
+            if is_tile(step - 5) and chunk_of_tile[step - 5][1] + chunk_of_tile[step - 5][2] - 1 == step - 5:
+                quantise_att(chunk_of_tile[step - 5][0])
+                waiting.extend([(chunk_of_tile[step - 5][0], cb) for cb in range(C_BLOCKS)])
             if step == 1:
                 quantise_v()
             if step == 5:
                 nc.vector.tensor_copy(out=gain_f32[:], in_=gain_bf[:])
             if is_tile(step - 1):
                 quantise_e(step - 1)
+            if late:
+                for chunk, cb in blocks:
+                    residual(chunk, cb)

@@ -174,7 +174,7 @@ def tile_selfattentionconv2d_pb_t_kernel(
         def row_max(i):
             half_max = half_maxes[i]
             minus_max = small.tile([P, 1], F32)
-            nc.vector.tensor_scalar(
+            nc.gpsimd.tensor_scalar(
                 out=minus_max[:],
                 in0=half_max[:, 0:1],
                 scalar1=half_max[:, 1:2],
@@ -228,7 +228,9 @@ def tile_selfattentionconv2d_pb_t_kernel(
 
         def add_row_sums(pair):
             row_sum = small.tile([P, PAIR], F32)
-            nc.vector.reduce_sum(out=row_sum[:], in_=e_sums[pair][:], axis=AXIS_X)
+            nc.gpsimd.tensor_tensor(
+                out=row_sum[:], in0=e_sums[pair][:, :, 0], in1=e_sums[pair][:, :, 1], op=ALU.add
+            )
             row_sums[pair] = row_sum
 
         def invert_row_sums(pair):

@@ -47,7 +47,7 @@ def tile_selfattentionconv2d_pb_t_kernel(
         small = stack.enter_context(tc.tile_pool(name="small", bufs=4))
         stream = stack.enter_context(tc.tile_pool(name="stream", bufs=3))
         packed = stack.enter_context(tc.tile_pool(name="packed", bufs=4))
-        results = stack.enter_context(tc.tile_pool(name="results", bufs=8))
+        results = stack.enter_context(tc.tile_pool(name="results", bufs=12))
         psum_scores = stack.enter_context(tc.psum_pool(name="psum_scores", bufs=2))
         psum_roles = stack.enter_context(tc.psum_pool(name="psum_roles", bufs=1))
 
@@ -279,7 +279,7 @@ def tile_selfattentionconv2d_pb_t_kernel(
             if place == 0:
                 att_grouped[chunk] = stream.tile([P, tiles * P * PACK], BF16, name="att_grp", align_bytes=64)
             words = att_grouped[chunk][:].bitcast(F32).rearrange("p (m n u) -> p m n u", m=tiles, u=2)
-            engine_copy = nc.scalar.copy if pair == 15 or pair % 4 == 0 else nc.vector.tensor_copy
+            engine_copy = nc.scalar.copy if pair >= 14 or pair % 4 == 0 else nc.vector.tensor_copy
             engine_copy(
                 out=words[:, place : place + PAIR, :, :],
                 in_=attT_banks[pair][:].rearrange("p (m u n) -> p m n u", m=PAIR, u=2),
@@ -345,9 +345,9 @@ def tile_selfattentionconv2d_pb_t_kernel(
             late = step >= N_TILES
             room = 2 * GROUP if late else GROUP
             blocks = []
-            while taken < len(waiting) and chunks[waiting[taken][0]][1] <= room:
+            while taken < len(waiting) and waiting[taken][2] <= step and chunks[waiting[taken][0]][1] <= room:
                 room -= chunks[waiting[taken][0]][1]
-                blocks.append(waiting[taken])
+                blocks.append(waiting[taken][:2])
                 taken += 1
             if is_tile(step):
                 exponentials(step)
@@ -379,17 +379,18 @@ def tile_selfattentionconv2d_pb_t_kernel(
                     regroup_v(t)
             if is_tile(step - 1):
                 regroup_e(step - 1)
+            if is_last_of(step - 4, PAIR):
+                regroup_att((step - 4) // PAIR)
             if is_tile(step - 2):
                 normalise(step - 2)
             if is_last_of(step, PAIR):
                 add_row_sums(step // PAIR)
-            if is_last_of(step - 4, PAIR):
-                regroup_att((step - 4) // PAIR)
             if is_last_of(step, PAIR):
                 invert_row_sums(step // PAIR)
             if is_tile(step - 5) and chunk_of_tile[step - 5][1] + chunk_of_tile[step - 5][2] - 1 == step - 5:
                 quantise_att(chunk_of_tile[step - 5][0])
-                waiting.extend([(chunk_of_tile[step - 5][0], cb) for cb in range(C_BLOCKS)])
+                ready = step + (1 if chunk_of_tile[step - 5][2] == GROUP else 2)
+                waiting.extend([(chunk_of_tile[step - 5][0], cb, ready) for cb in range(C_BLOCKS)])
             if step == 1:
                 quantise_v()
             if step == 5:

@@ -323,7 +323,8 @@ def tile_selfattentionconv2d_pb_t_kernel(
                 op0=ALU.mult,
                 op1=ALU.add,
             )
-            nc.sync.dma_start(out=out_rows[:, cb, pixels], in_=o_sb[:])
+            queue = nc.scalar if tiles == PAIR and cb % 2 == 1 else nc.sync
+            queue.dma_start(out=out_rows[:, cb, pixels], in_=o_sb[:])
 
         def is_tile(i):
             return 0 <= i < N_TILES

from contextlib import ExitStack

import concourse.mybir as mybir
from concourse.masks import make_identity

F32 = mybir.dt.float32
BF16 = mybir.dt.bfloat16
I32 = mybir.dt.int32
U32 = mybir.dt.uint32
U8 = mybir.dt.uint8
FP8X4 = mybir.dt.float8_e4m3fn_x4
ALU = mybir.AluOpType
ACT = mybir.ActivationFunctionType
AXIS_X = mybir.AxisListType.X

P = 128
PACK = 4
K_PASS = P * PACK
BANK = 512

N_PIX = 4096
N_POS = 1024
D_QK = 128
D_V = 512
C_OUT = 512

N_TILES = N_PIX // P
GROUP = 4
N_GROUPS = N_TILES // GROUP
POS_PASSES = N_POS // K_PASS
POS_HALVES = N_POS // BANK
V_BLOCKS = D_V // P
C_BLOCKS = C_OUT // P

PAIR = 2
ROLES = ("eT", "att", "attT", "y")

FLOPS = 2 * N_PIX * N_POS * D_QK + 2 * N_PIX * N_POS * D_V + 2 * N_PIX * D_V * C_OUT


def tile_selfattentionconv2d_pb_t_kernel(
    tc, q, k_pool, v_pool, imgs, w_out_words, w_out_scales, gain, out
):
    nc = tc.nc
    with ExitStack() as stack:
        keep = stack.enter_context(tc.tile_pool(name="keep", bufs=1))
        small = stack.enter_context(tc.tile_pool(name="small", bufs=4))
        stream = stack.enter_context(tc.tile_pool(name="stream", bufs=3))
        packed = stack.enter_context(tc.tile_pool(name="packed", bufs=4))
        results = stack.enter_context(tc.tile_pool(name="results", bufs=12))
        psum_scores = stack.enter_context(tc.psum_pool(name="psum_scores", bufs=2))
        psum_roles = stack.enter_context(tc.psum_pool(name="psum_roles", bufs=1))

        k_sb = keep.tile([P, N_POS], BF16)
        nc.sync.dma_start(out=k_sb[:], in_=k_pool.rearrange("b d m -> (b d) m"))
        q_sb = keep.tile([P, N_PIX], BF16)
        q_rows = q.rearrange("b d n -> (b d) n")
        first = GROUP * P
        nc.sync.dma_start(out=q_sb[:, :first], in_=q_rows[:, :first])
        v_sb = keep.tile([P, V_BLOCKS, N_POS], BF16)
        nc.sync.dma_start(out=v_sb[:], in_=v_pool.rearrange("b (t j) m -> j (b t) m", j=P))
        nc.sync.dma_start(out=q_sb[:, first:], in_=q_rows[:, first:])
        gain_bf = keep.tile([P, 1], BF16)
        nc.sync.dma_start(out=gain_bf[:], in_=gain.partition_broadcast(P))
        w_words = keep.tile([P, C_OUT * PACK], U8, align_bytes=64)
        nc.sync.dma_start(
            out=w_words[:].bitcast(I32),
            in_=w_out_words.rearrange("g p c t -> (g p) (c t)").bitcast(I32),
        )
        w_scales = keep.tile([P, C_OUT], U8, align_bytes=64)
        nc.vector.memset(w_scales[:].bitcast(I32), 0)
        scale_rows = w_out_scales.rearrange("g r c -> (g r) c")
        for quadrant in range(4):
            nc.sync.dma_start(
                out=w_scales[32 * quadrant : 32 * quadrant + 4, :].bitcast(I32),
                in_=scale_rows[4 * quadrant : 4 * quadrant + 4, :].bitcast(I32),
            )
        imgs_sb = keep.tile([P, C_BLOCKS, N_PIX], BF16)
        imgs_rows = imgs.rearrange("b (cb c) h w -> c (b cb) (h w)", c=P)
        for cb in range(C_BLOCKS):
            nc.sync.dma_start(out=imgs_sb[:, cb, :], in_=imgs_rows[:, cb, :])
        out_rows = out.rearrange("b (cb c) h w -> c (b cb) (h w)", c=P)

        ident = keep.tile([P, P], F32)
        make_identity(nc, ident[:])
        gain_f32 = keep.tile([P, 1], F32)

        k_sorted = keep.tile([P, N_POS], BF16)
        nc.vector.tensor_copy(
            out=k_sorted[:].bitcast(F32).rearrange("d (g u p) -> d g u p", g=POS_PASSES, u=2),
            in_=k_sb[:].bitcast(F32).rearrange("d (g p u) -> d g u p", g=POS_PASSES, u=2),
        )

        v_grouped = keep.tile([P, POS_PASSES, V_BLOCKS, P, PACK], BF16, align_bytes=64)
        v_grouped_words = v_grouped[:].rearrange("p g t j k -> p (g t j k)").bitcast(F32)
        v_grouped_words = v_grouped_words.rearrange(
            "p (g t j u) -> p g t j u", g=POS_PASSES, t=V_BLOCKS, u=2
        )
        v_banks = {}
        late_banks = []

        def product_bank(role, late):
            if late:
                late_banks.append(role)
                return psum_scores.tile([P, BANK], F32, name="s_ps%d" % (len(late_banks) % POS_HALVES))
            return psum_roles.tile([P, BANK], F32, name=role)

        v_codes = keep.tile([P, POS_PASSES, V_BLOCKS, P], U32, align_bytes=64)
        v_scales = keep.tile([P, POS_PASSES, V_BLOCKS, P], U8, align_bytes=64)

        def transpose_v(t):
            v_words_in = v_sb[:, t, :].bitcast(F32)
            vT_ps = psum_roles.tile([P, POS_PASSES * 2, P], F32, tag=ROLES[t])
            for g in range(POS_PASSES):
                for u in range(2):
                    nc.tensor.transpose(
                        vT_ps[:, 2 * g + u, :],
                        v_words_in[:, 256 * g + u : 256 * (g + 1) : 2],
                        ident[:],
                    )
            v_banks[t] = vT_ps

        def regroup_v(t):
            engine_copy = nc.scalar.copy if t < 0 else nc.vector.tensor_copy
            engine_copy(
                out=v_grouped_words[:, :, t, :, :],
                in_=v_banks[t][:].rearrange("p (g u) j -> p g j u", u=2),
            )

        def quantise_v():
            nc.vector.quantize_mx(
                out=v_codes[:].rearrange("p g t j -> p (g t j)").bitcast(FP8X4),
                scales=v_scales[:].rearrange("p g t j -> p (g t j)"),
                in_=v_grouped[:].rearrange("p g t j k -> p (g t j k)"),
            )

        score_banks = {}
        half_maxes = {}
        neg_max = {}
        row_sums = {}
        e_rows = {}
        e_sums = {}
        e_banks = {}
        e_grouped = {}
        e_packed = {}
        inv_sum = {}
        att_banks = {}
        att_rows = {}
        attT_banks = {}
        att_grouped = {}
        att_packed = {}
        y_banks = {}

        def scores(i):
            halves = []
            for h in range(POS_HALVES):
                s_ps = psum_scores.tile([P, BANK], F32, name="s_ps%d" % h)
                nc.tensor.matmul(
                    out=s_ps[:],
                    lhsT=q_sb[:, P * i : P * (i + 1)],
                    rhs=k_sorted[:, BANK * h : BANK * (h + 1)],
                    start=True,
                    stop=True,
                )
                halves.append(s_ps)
            score_banks[i] = halves

        def half_maxima(i):
            half_max = small.tile([P, POS_HALVES], F32)
            for h in range(POS_HALVES):
                nc.vector.reduce_max(out=half_max[:, h : h + 1], in_=score_banks[i][h][:], axis=AXIS_X)
            half_maxes[i] = half_max

        def row_max(i):
            half_max = half_maxes[i]
            minus_max = small.tile([P, 1], F32)
            nc.gpsimd.tensor_scalar(
                out=minus_max[:],
                in0=half_max[:, 0:1],
                scalar1=half_max[:, 1:2],
                scalar2=-1.0,
                op0=ALU.max,
                op1=ALU.mult,
            )
            neg_max[i] = minus_max

        def exponentials(i):
            pair, member = divmod(i, PAIR)
            if member == 0:
                e_sums[pair] = small.tile([P, PAIR, POS_HALVES], F32, name="sums")
            e_bf = stream.tile([P, N_POS], BF16)
            for h in range(POS_HALVES):
                nc.scalar.activation(
                    out=e_bf[:, BANK * h : BANK * (h + 1)],
                    in_=score_banks[i][h][:],
                    func=ACT.Exp,
                    bias=neg_max[i][:, 0:1],
                    scale=1.0,
                    accum_out=e_sums[pair][:, member, h : h + 1],
                )
            e_rows[i] = e_bf

        def transpose_e(i):
            eT_ps = product_bank("eT", i >= N_TILES - 1)
            words = e_rows[i][:].bitcast(F32)
            for b in range(POS_PASSES * 2):
                nc.tensor.transpose(eT_ps[:, P * b : P * (b + 1)], words[:, P * b : P * (b + 1)], ident[:])
            e_banks[i] = eT_ps

        def regroup_e(i):
            e_grp = stream.tile([P, POS_PASSES * P * PACK], BF16, align_bytes=64)
            engine_copy = nc.vector.tensor_copy if 2 <= i < 6 else nc.scalar.copy
            engine_copy(
                out=e_grp[:].bitcast(F32).rearrange("p (g n u) -> p g n u", g=POS_PASSES, u=2),
                in_=e_banks[i][:].rearrange("p (g u n) -> p g n u", g=POS_PASSES, u=2),
            )
            e_grouped[i] = e_grp

        def quantise_e(i):
            e_codes = packed.tile([P, POS_PASSES, P], U32, align_bytes=64)
            e_scales = packed.tile([P, POS_PASSES, P], U8, align_bytes=64)
            nc.vector.quantize_mx(
                out=e_codes[:].rearrange("p g n -> p (g n)").bitcast(FP8X4),
                scales=e_scales[:].rearrange("p g n -> p (g n)"),
                in_=e_grouped[i][:],
            )
            e_packed[i] = (e_codes, e_scales)

        def add_row_sums(pair):
            row_sum = small.tile([P, PAIR], F32)
            nc.gpsimd.tensor_tensor(
                out=row_sum[:], in0=e_sums[pair][:, :, 0], in1=e_sums[pair][:, :, 1], op=ALU.add
            )
            row_sums[pair] = row_sum

        def invert_row_sums(pair):
            inverse = small.tile([P, PAIR], F32)
            nc.vector.reciprocal(out=inverse[:], in_=row_sums[pair][:])
            inv_sum[pair] = inverse

        def attend(i):
            e_codes, e_scales = e_packed[i]
            att_ps = product_bank("att", i >= N_TILES - 2)
            for g in range(POS_PASSES):
                nc.tensor.matmul_mx(
                    out=att_ps[:],
                    lhsT=e_codes[:, g, :].bitcast(FP8X4),
                    lhsT_scale=e_scales[:, g, :],
                    rhs=v_codes[:, g, :, :].rearrange("p t j -> p (t j)").bitcast(FP8X4),
                    rhs_scale=v_scales[:, g, :, :].rearrange("p t j -> p (t j)"),
                    start=(g == 0),
                    stop=(g == POS_PASSES - 1),
                )
            att_banks[i] = att_ps

        def normalise(i):
            pair, member = divmod(i, PAIR)
            att_bf = stream.tile([P, D_V], BF16)
            nc.scalar.activation(
                out=att_bf[:].rearrange("n (u p e) -> n u p e", u=2, e=2),
                in_=att_banks[i][:].rearrange("n (p u e) -> n u p e", u=2, e=2),
                func=ACT.Copy,
                scale=inv_sum[pair][:, member : member + 1],
            )
            att_rows[i] = att_bf

        def transpose_att(pair):
            attT_ps = product_bank("attT", False)
            for member in range(PAIR):
                words = att_rows[PAIR * pair + member][:].bitcast(F32)
                for u in range(2):
                    place = P * (2 * member + u)
                    nc.tensor.transpose(attT_ps[:, place : place + P], words[:, P * u : P * (u + 1)], ident[:])
            attT_banks[pair] = attT_ps

        def regroup_att(pair):
            chunk, first_tile, tiles = chunk_of_tile[PAIR * pair]
            place = PAIR * pair - first_tile
            if place == 0:
                att_grouped[chunk] = stream.tile([P, tiles * P * PACK], BF16, name="att_grp", align_bytes=64)
            words = att_grouped[chunk][:].bitcast(F32).rearrange("p (m n u) -> p m n u", m=tiles, u=2)
            engine_copy = nc.scalar.copy if pair >= 14 or pair % 4 == 0 else nc.vector.tensor_copy
            engine_copy(
                out=words[:, place : place + PAIR, :, :],
                in_=attT_banks[pair][:].rearrange("p (m u n) -> p m n u", m=PAIR, u=2),
            )

        def quantise_att(chunk):
            tiles = chunks[chunk][1]
            att_codes = stream.tile([P, tiles * P], U32, align_bytes=64)
            att_scales = stream.tile([P, tiles * P], U8, align_bytes=64)
            nc.vector.quantize_mx(
                out=att_codes[:].bitcast(FP8X4),
                scales=att_scales[:],
                in_=att_grouped[chunk][:],
            )
            att_packed[chunk] = (att_codes, att_scales)

        def project(chunk, cb, late):
            att_codes, att_scales = att_packed[chunk]
            tiles = chunks[chunk][1]
            y_ps = product_bank("y", late)
            nc.tensor.matmul_mx(
                out=y_ps[:, : tiles * P],
                lhsT=w_words[:, P * PACK * cb : P * PACK * (cb + 1)].bitcast(FP8X4),
                lhsT_scale=w_scales[:, P * cb : P * (cb + 1)],
                rhs=att_codes[:].bitcast(FP8X4),
                rhs_scale=att_scales[:],
                start=True,
                stop=True,
            )
            y_banks[(chunk, cb)] = y_ps

        def residual(chunk, cb):
            first_tile, tiles = chunks[chunk]
            pixels = slice(P * first_tile, P * (first_tile + tiles))
            o_sb = results.tile([P, tiles * P], F32)
            nc.vector.scalar_tensor_tensor(
                out=o_sb[:],
                in0=y_banks[(chunk, cb)][:, : tiles * P],
                scalar=gain_f32[:, 0:1],
                in1=imgs_sb[:, cb, pixels],
                op0=ALU.mult,
                op1=ALU.add,
            )
            queue = nc.scalar if tiles == PAIR and cb % 2 == 1 else nc.sync
            queue.dma_start(out=out_rows[:, cb, pixels], in_=o_sb[:])

        def is_tile(i):
            return 0 <= i < N_TILES

        def is_last_of(i, count):
            return is_tile(i) and i % count == count - 1

        chunks = [(GROUP * g, GROUP) for g in range(N_GROUPS - 1)]
        chunks.extend([(N_TILES - GROUP + PAIR * h, PAIR) for h in range(GROUP // PAIR)])
        chunk_of_tile = {}
        for chunk, (first_tile, tiles) in enumerate(chunks):
            for i in range(first_tile, first_tile + tiles):
                chunk_of_tile[i] = (chunk, first_tile, tiles)
        waiting = []
        taken = 0

        stack.enter_context(tc.manual_schedule())
        for step in range(-2, N_TILES + 16):
            late = step >= N_TILES
            room = 2 * GROUP if late else GROUP
            blocks = []
            while taken < len(waiting) and waiting[taken][2] <= step and chunks[waiting[taken][0]][1] <= room:
                room -= chunks[waiting[taken][0]][1]
                blocks.append(waiting[taken][:2])
                taken += 1
            if is_tile(step):
                exponentials(step)
            if is_tile(step - 1):
                transpose_e(step - 1)
            for chunk, cb in blocks:
                project(chunk, cb, late)
            if is_tile(step - 2):
                attend(step - 2)
            if is_last_of(step - 3, PAIR):
                transpose_att((step - 3) // PAIR)
            if is_tile(step + 2):
                scores(step + 2)
            for t in range(V_BLOCKS):
                if step == (t // 2) - 1:
                    transpose_v(t)
            for t in range(V_BLOCKS):
                if step == t // 2 and t < 0:
                    regroup_v(t)
            if is_tile(step + 1):
                half_maxima(step + 1)
            if not late:
                for chunk, cb in blocks:
                    residual(chunk, cb)
            if is_tile(step + 1):
                row_max(step + 1)
            for t in range(V_BLOCKS):
                if step == t // 2 and t >= 0:
                    regroup_v(t)
            if is_tile(step - 1):
                regroup_e(step - 1)
            if is_last_of(step - 4, PAIR):
                regroup_att((step - 4) // PAIR)
            if is_tile(step - 2):
                normalise(step - 2)
            if is_last_of(step, PAIR):
                add_row_sums(step // PAIR)
            if is_last_of(step, PAIR):
                invert_row_sums(step // PAIR)
            if is_tile(step - 5) and chunk_of_tile[step - 5][1] + chunk_of_tile[step - 5][2] - 1 == step - 5:
                quantise_att(chunk_of_tile[step - 5][0])
                ready = step + (1 if chunk_of_tile[step - 5][2] == GROUP else 2)
                waiting.extend([(chunk_of_tile[step - 5][0], cb, ready) for cb in range(C_BLOCKS)])
            if step == 1:
                quantise_v()
            if step == 5:
                nc.vector.tensor_copy(out=gain_f32[:], in_=gain_bf[:])
            if is_tile(step - 1):
                quantise_e(step - 1)
            if late:
                for chunk, cb in blocks:
                    residual(chunk, cb)
